import numpy as np
import ml_dtypes


def mxq(x, axis, fmt="e4m3"):
    dtype, down = {"e4m3": (ml_dtypes.float8_e4m3fn, 7), "e5m2": (ml_dtypes.float8_e5m2, 14)}[fmt]
    v = np.moveaxis(np.asarray(x, np.float32).astype(ml_dtypes.bfloat16).astype(np.float64), axis, -1)
    blocks = v.reshape(v.shape[:-1] + (-1, 32))
    amax = np.abs(blocks).max(-1, keepdims=True)
    byte = np.maximum(np.where(amax > 0, np.frexp(amax)[1] - 1 + 127, 0) - down, 1)
    scale = np.exp2(byte - 127.0)
    codes = (blocks / scale).astype(np.float32).astype(dtype).astype(np.float64)
    return np.moveaxis((codes * scale).reshape(v.shape), -1, axis)


WIDE = False


def mx_kscale(k):
    if not WIDE:
        return np.ones(k)
    levels = np.array([10, -10, 5, -5, 0])
    if k % 512:
        return np.exp2(np.random.permutation(np.resize(levels, k // 32))).repeat(32)
    a = np.empty((k // 512, 16))
    for p in range(k // 512):
        a[p, :8] = np.random.permutation(np.resize(levels, 8))
        for g in range(8):
            far = levels[np.abs(levels - a[p, g]) >= 10]
            a[p, g + 8] = far[np.random.randint(len(far))]
    return np.exp2(a.ravel()).repeat(32)


BF16 = ml_dtypes.bfloat16


def bf(x):
    return np.asarray(x, np.float32).astype(BF16)


def f64(x):
    return np.asarray(x).astype(np.float64)


B, S, H, D = 4, 64, 16, 128
T = B * S
HID = H * D
D2 = D // 2
ROPE_THETA = 10000.0


def rotary(x, cos, sin):
    x1, x2 = x[..., :D2], x[..., D2:]
    c, s = cos[:, None, :], sin[:, None, :]
    return np.concatenate([x1 * c - x2 * s, x2 * c + x1 * s], axis=-1)


def draw0():
    s = mx_kscale(HID)
    pos = np.tile(np.arange(S, dtype=np.float64), B)
    inv_freq = 1.0 / ROPE_THETA ** (np.arange(0, D, 2, dtype=np.float64) / D)
    freqs = pos[:, None] * inv_freq[None, :]
    return {"hidden_states": bf(np.random.standard_normal((T, HID)) * s),
            "cos": bf(np.cos(freqs)),
            "sin": bf(np.sin(freqs)),
            "w_qkv": bf(np.random.standard_normal((3 * HID, HID)) / np.sqrt(HID) / s[None, :]),
            "b_qkv": bf(np.random.standard_normal(3 * HID) * 0.3)}


def core(hidden_states, cos, sin, w_qkv, b_qkv):
    proj = mxq(f64(hidden_states), 1, "e4m3") @ mxq(f64(w_qkv), 1, "e4m3").T
    qkv = (proj + f64(b_qkv)).reshape(T, 3, H, D)
    q = rotary(qkv[:, 0], f64(cos), f64(sin))
    k = rotary(qkv[:, 1], f64(cos), f64(sin))
    v = qkv[:, 2]
    return q, k, v


def e4m3fn_bytes(y):
    return np.clip(np.asarray(y, np.float64), -448.0, 448.0).astype(np.float32).astype(ml_dtypes.float8_e4m3fn).view(np.uint8)


def e4m3fn_values(b):
    return np.asarray(b, np.uint8).view(ml_dtypes.float8_e4m3fn).astype(np.float64)


def setup_inputs():
    d = draw0()
    x0 = np.asarray(d['w_qkv']).astype(np.float64)
    s = (np.max(np.abs(x0), axis=(0,), keepdims=True) / 448.0).astype(np.float32)
    out = {}
    for k, v in d.items():
        if k == 'w_qkv':
            out['w_qkv_bytes'] = e4m3fn_bytes(x0 / s.astype(np.float64))
            out['w_qkv_scale'] = s
        else:
            out[k] = v
    return out


def reference(hidden_states, cos, sin, w_qkv_bytes, w_qkv_scale, b_qkv):
    return core(hidden_states, cos, sin, e4m3fn_values(w_qkv_bytes) * w_qkv_scale.astype(np.float64), b_qkv)

@@ -1,0 +1,318 @@
+from contextlib import ExitStack
+
+import concourse.mybir as mybir
+from concourse.masks import make_identity
+
+TOKENS = 256
+HID = 2048
+HEADS = 16
+D = 128
+HALF = D // 2
+TILES = 3 * HEADS
+
+FLOPS = 2 * TOKENS * 3 * HID * HID
+
+F32 = mybir.dt.float32
+BF16 = mybir.dt.bfloat16
+U32 = mybir.dt.uint32
+U8 = mybir.dt.uint8
+FP8 = mybir.dt.float8_e4m3fn
+FP8X4 = mybir.dt.float8_e4m3fn_x4
+ACT = mybir.ActivationFunctionType
+ALU = mybir.AluOpType
+
+P = 128
+PACK = 4
+K_PASS = P * PACK
+PASSES = HID // K_PASS
+WORDS_PASS = K_PASS // 2
+GROUP = 4
+
+COPIES = 2
+N_MOVING = COPIES * TOKENS
+
+ORDER = list(range(2 * HEADS, TILES)) + list(range(2 * HEADS))
+FIRST = ORDER[0]
+LAST = ORDER[TILES - 1]
+
+
+def has_rope(j):
+    return j < 2 * HEADS
+
+
+def scalar_passes(j):
+    if has_rope(j):
+        return 1 if j % 2 == 0 else 0
+    return 1 if j % 4 == 1 else 0
+
+
+def tile_flashneoxattention_pa_kernel(
+    tc, hidden_states, cos, sin, w_qkv_bytes, w_qkv_scale, b_qkv, out_0, out_1, out_2
+):
+    nc = tc.nc
+    outs = (out_0, out_1, out_2)
+
+    with ExitStack() as ctx:
+        const = ctx.enter_context(tc.tile_pool(name="const", bufs=1))
+        byte_pool = ctx.enter_context(tc.tile_pool(name="byte_pool", bufs=TILES))
+        work = ctx.enter_context(tc.tile_pool(name="work", bufs=3))
+        ps_words = ctx.enter_context(tc.psum_pool(name="ps_words", bufs=4))
+        ps_sums = ctx.enter_context(tc.psum_pool(name="ps_sums", bufs=2))
+        ps_done = ctx.enter_context(tc.psum_pool(name="ps_done", bufs=2))
+        ctx.enter_context(tc.manual_schedule())
+
+        scale_rows = const.tile([P, HID], F32, name="scale_rows")
+        scale_vec = w_qkv_scale.rearrange("o k -> (o k)")
+        for g in range(PASSES):
+            cols = slice(g * K_PASS, (g + 1) * K_PASS)
+            nc.scalar.dma_start(out=scale_rows[:, cols], in_=scale_vec[cols].partition_broadcast(P))
+
+        scale_cols = const.tile([P, PASSES, PACK], F32, name="scale_cols")
+        nc.scalar.dma_start(out=scale_cols[:], in_=w_qkv_scale.rearrange("o (g p t) -> p (o g) t", p=P, t=PACK))
+
+        w_bytes = {}
+        for j in ORDER:
+            byte_tile = byte_pool.tile([P, HID], U8, name="byte_tile", tag="w_bytes")
+            w_bytes[j] = byte_tile
+        x_rows = const.tile([P, 2, HID], BF16, name="x_rows")
+        for n in range(TILES):
+            j = ORDER[n]
+            if n == 2:
+                nc.sync.dma_start(out=x_rows[:], in_=hidden_states.rearrange("(a p) k -> p a k", p=P))
+            nc.sync.dma_start(out=w_bytes[j][:], in_=w_qkv_bytes[j * P : (j + 1) * P, :])
+
+        bias_rows = const.tile([P, P], BF16, name="bias_rows")
+        nc.vector.memset(bias_rows[:], 0.0)
+        nc.scalar.dma_start(out=bias_rows[0:TILES, :], in_=b_qkv.rearrange("(j p) -> j p", p=P))
+
+        trig = const.tile([P, 2, 4, HALF], BF16, name="trig")
+        cos_view = cos.rearrange("(a p) d -> p a d", p=P)
+        sin_view = sin.rearrange("(a p) d -> p a d", p=P)
+        nc.scalar.dma_start(out=trig[:, :, 0, :], in_=cos_view)
+        nc.scalar.dma_start(out=trig[:, :, 1, :], in_=cos_view)
+        nc.scalar.dma_start(out=trig[:, :, 2, :], in_=sin_view)
+        nc.scalar.dma_start(out=trig[:, :, 3, :], in_=sin_view)
+
+        ident = const.tile([P, P], F32, name="ident")
+        make_identity(nc, ident[:])
+        ident_bf = const.tile([P, P], BF16, name="ident_bf")
+        make_identity(nc, ident_bf[:])
+        swap_halves = const.tile([P, P], F32, name="swap_halves")
+        nc.vector.tensor_copy(out=swap_halves[:, 0:HALF], in_=ident[:, HALF:P])
+        nc.vector.tensor_copy(out=swap_halves[:, HALF:P], in_=ident[:, 0:HALF])
+
+        x_codes = const.tile([P, PASSES * N_MOVING], U32, name="x_codes", align_bytes=64)
+        x_scales = const.tile([P, PASSES * N_MOVING], U8, name="x_scales", align_bytes=64)
+        x_packed = const.tile([P, PASSES, TOKENS * PACK], BF16, name="x_packed", align_bytes=64)
+        bias = const.tile([P, TILES], F32, name="bias")
+        tables = const.tile([P, COPIES, TOKENS], F32, name="tables")
+
+        tiles = {}
+
+        def scale_product(j):
+            w_rows = work.tile([P, HID], BF16, name="w_rows", tag="w_rows")
+            split = (PASSES - scalar_passes(j)) * K_PASS
+            if split < HID:
+                nc.scalar.copy(out=w_rows[:, split:HID], in_=w_bytes[j][:, split:HID].bitcast(FP8))
+            pieces = 1
+            if j == FIRST:
+                pieces = split // K_PASS
+            if j == LAST:
+                pieces = 2
+            width = split // pieces
+            for c in range(pieces):
+                cols = slice(c * width, (c + 1) * width)
+                nc.vector.tensor_tensor(
+                    out=w_rows[:, cols], in0=w_bytes[j][:, cols].bitcast(FP8), in1=scale_rows[:, cols], op=ALU.mult
+                )
+            tiles[("w_rows", j)] = w_rows
+
+        def transpose_pass(dst, words, g, u):
+            nc.tensor.transpose(dst, words[:, WORDS_PASS * g + u : WORDS_PASS * (g + 1) : 2], ident[:])
+
+        def turn(j):
+            words = tiles[("w_rows", j)][:].bitcast(F32)
+            w_packed = work.tile([P, PASSES * P * PACK], BF16, name="w_packed", tag="w_packed", align_bytes=64)
+            packed_words = w_packed[:].bitcast(F32).rearrange("p (g r u) -> p g r u", g=PASSES, u=2)
+            packed_vals = w_packed[:].rearrange("p (g r t) -> p g r t", g=PASSES, t=PACK)
+            for b in range(2):
+                bank = ps_words.tile([P, 2, 2, P], F32, name="bank", tag="words")
+                for gl in range(2):
+                    for u in range(2):
+                        transpose_pass(bank[:, gl, u, :], words, 2 * b + gl, u)
+                scaled = max(0, min(2, PASSES - scalar_passes(j) - 2 * b))
+                if scaled > 0:
+                    nc.scalar.copy(
+                        out=packed_words[:, 2 * b : 2 * b + scaled],
+                        in_=bank[:, 0:scaled].rearrange("p g u r -> p g r u"),
+                    )
+                for gl in range(scaled, 2):
+                    g = 2 * b + gl
+                    planes = work.tile([P, PACK, P], BF16, name="planes", tag="planes")
+                    for t in range(PACK):
+                        nc.scalar.activation(
+                            out=planes[:, t, :],
+                            in_=bank[:, gl, t // 2, :].bitcast(BF16).rearrange("p (r e) -> p r e", e=2)[:, :, t % 2],
+                            func=ACT.Copy,
+                            scale=scale_cols[:, g, t : t + 1],
+                        )
+                    nc.scalar.copy(out=packed_vals[:, g], in_=planes[:].rearrange("p t r -> p r t"))
+            tiles[("w_packed", j)] = w_packed
+
+        def quantise(j):
+            w_codes = work.tile([P, PASSES * P], U32, name="w_codes", tag="w_codes", align_bytes=64)
+            w_scales = work.tile([P, PASSES * P], U8, name="w_scales", tag="w_scales", align_bytes=64)
+            pieces = 2 if j == LAST else 1
+            width = PASSES * P // pieces
+            for c in range(pieces):
+                cols = slice(c * width, (c + 1) * width)
+                nc.vector.quantize_mx(
+                    out=w_codes[:, cols].bitcast(FP8X4),
+                    scales=w_scales[:, cols],
+                    in_=tiles[("w_packed", j)][:, PACK * c * width : PACK * (c + 1) * width],
+                )
+            tiles[("w_codes", j)] = (w_codes, w_scales)
+
+        def multiply(j, half):
+            w_codes, w_scales = tiles[("w_codes", j)]
+            if half == 0:
+                new_sums = ps_sums.tile([P, N_MOVING], F32, name="new_sums", tag="sums")
+                tiles[("sums", j)] = new_sums
+            sums = tiles[("sums", j)]
+            for g in (2 * half, 2 * half + 1):
+                rows = slice(g * P, (g + 1) * P)
+                toks = slice(g * N_MOVING, (g + 1) * N_MOVING)
+                nc.tensor.matmul_mx(
+                    out=sums[:],
+                    lhsT=w_codes[:, rows].bitcast(FP8X4),
+                    lhsT_scale=w_scales[:, rows],
+                    rhs=x_codes[:, toks].bitcast(FP8X4),
+                    rhs_scale=x_scales[:, toks],
+                    start=(g == 0),
+                    stop=(g == PASSES - 1),
+                )
+            if half == 1 and not has_rope(j):
+                v_head = work.tile([P, TOKENS], F32, name="v_head", tag="v_head")
+                nc.scalar.activation(
+                    out=v_head[:], in_=sums[:, 0:TOKENS], func=ACT.Identity, bias=bias[:, j : j + 1], scale=1.0
+                )
+                tiles[("v_head", j)] = v_head
+
+        def rope_products(j):
+            if has_rope(j):
+                products = work.tile([P, COPIES, TOKENS], F32, name="products", tag="products")
+                nc.vector.scalar_tensor_tensor(
+                    out=products[:].rearrange("p c n -> p (c n)"),
+                    in0=tiles[("sums", j)][:],
+                    scalar=bias[:, j : j + 1],
+                    in1=tables[:].rearrange("p c n -> p (c n)"),
+                    op0=ALU.add,
+                    op1=ALU.mult,
+                )
+                tiles[("products", j)] = products
+
+        def store_group(j, a, staged):
+            first_head = (j % HEADS) - (GROUP - 1)
+            nc.sync.dma_start(
+                out=outs[j // HEADS][a * P : (a + 1) * P, first_head : first_head + GROUP, :].rearrange(
+                    "t h d -> t (h d)"
+                ),
+                in_=staged[:],
+            )
+
+        def finish(j):
+            place = j % GROUP
+            if place == 0:
+                done_0 = ps_done.tile([P, GROUP * D], F32, name="done_0", tag="done")
+                done_1 = ps_done.tile([P, GROUP * D], F32, name="done_1", tag="done")
+                tiles["done"] = (done_0, done_1)
+            done = tiles["done"]
+            for a in range(2):
+                dst = done[a][:, place * D : (place + 1) * D]
+                toks = slice(a * P, (a + 1) * P)
+                if has_rope(j):
+                    products = tiles[("products", j)]
+                    nc.tensor.matmul(
+                        dst, lhsT=products[:, 0, toks], rhs=ident[:], is_transpose=True, start=True, stop=False
+                    )
+                    nc.tensor.matmul(
+                        dst, lhsT=products[:, 1, toks], rhs=swap_halves[:], is_transpose=True, start=False, stop=True
+                    )
+                else:
+                    nc.tensor.transpose(dst, tiles[("v_head", j)][:, toks], ident[:])
+            ready = (GROUP - 1) * D
+            if j == LAST - 1:
+                for a in range(2):
+                    early = work.tile([P, GROUP * D], F32, name="early", tag="staged")
+                    nc.scalar.copy(out=early[:, 0:ready], in_=done[a][:, 0:ready])
+                    tiles[("staged", a)] = early
+            if j == LAST:
+                nc.scalar.copy(out=tiles[("staged", 0)][:, ready : GROUP * D], in_=done[0][:, ready : GROUP * D])
+                store_group(j, 0, tiles[("staged", 0)])
+                nc.vector.tensor_copy(out=tiles[("staged", 1)][:, ready : GROUP * D], in_=done[1][:, ready : GROUP * D])
+                store_group(j, 1, tiles[("staged", 1)])
+            elif place == GROUP - 1:
+                for a in range(2):
+                    staged = work.tile([P, GROUP * D], F32, name="staged", tag="staged")
+                    nc.scalar.copy(out=staged[:], in_=done[a][:])
+                    store_group(j, a, staged)
+
+        def turn_tokens():
+            for g in range(PASSES):
+                bank = ps_words.tile([P, 2, TOKENS], F32, name="bank", tag="words")
+                for a in range(2):
+                    words = x_rows[:, a, :].bitcast(F32)
+                    for u in range(2):
+                        transpose_pass(bank[:, u, a * P : (a + 1) * P], words, g, u)
+                nc.scalar.copy(
+                    out=x_packed[:, g, :].bitcast(F32).rearrange("p (r u) -> p r u", u=2),
+                    in_=bank[:].rearrange("p u r -> p r u"),
+                )
+
+        def quantise_tokens():
+            for block in range(PASSES * COPIES):
+                cols = slice(block * TOKENS, (block + 1) * TOKENS)
+                nc.vector.quantize_mx(
+                    out=x_codes[:, cols].bitcast(FP8X4), scales=x_scales[:, cols], in_=x_packed[:, block // COPIES, :]
+                )
+
+        def make_tables():
+            bias_bank = ps_words.tile([P, P], BF16, name="bias_bank", tag="words")
+            nc.tensor.transpose(bias_bank[:], bias_rows[:], ident_bf[:])
+            nc.scalar.copy(out=bias[:], in_=bias_bank[:, 0:TILES])
+            nc.scalar.activation(out=trig[:, :, 3, :], in_=trig[:, :, 3, :], func=ACT.Copy, scale=-1.0)
+            trig_bank = ps_words.tile([P, COPIES, TOKENS], BF16, name="trig_bank", tag="words")
+            for c in range(COPIES):
+                for a in range(2):
+                    nc.tensor.transpose(
+                        trig_bank[:, c, a * P : (a + 1) * P],
+                        trig[:, a, 2 * c : 2 * c + 2, :].rearrange("p c d -> p (c d)"),
+                        ident_bf[:],
+                    )
+            nc.scalar.copy(out=tables[:], in_=trig_bank[:])
+
+        def at(n):
+            return ORDER[n] if 0 <= n < TILES else None
+
+        for i in range(TILES + 5):
+            if at(i) is not None:
+                scale_product(at(i))
+            if i == TILES:
+                turn(at(i - 1))
+            if at(i - 3) is not None:
+                multiply(at(i - 3), 0)
+            if at(i - 1) is not None and i != TILES:
+                turn(at(i - 1))
+            if i == 1:
+                turn_tokens()
+                make_tables()
+            if at(i - 3) is not None:
+                multiply(at(i - 3), 1)
+            if at(i - 4) is not None:
+                rope_products(at(i - 4))
+            if i == 2:
+                quantise_tokens()
+            if at(i - 2) is not None:
+                quantise(at(i - 2))
+            if at(i - 5) is not None:
+                finish(at(i - 5))

@@ -42,8 +42,8 @@ def has_rope(j):
 
 def scalar_passes(j):
     if has_rope(j):
-        return 1 if j % 2 == 0 else 0
-    return 1 if j % 4 == 1 else 0
+        return 1 if j % 4 != 3 else 0
+    return 1 if j % 2 == 1 else 0
 
 
 def tile_flashneoxattention_pa_kernel(
@@ -148,15 +148,18 @@ def tile_flashneoxattention_pa_kernel(
                     )
                 for gl in range(scaled, 2):
                     g = 2 * b + gl
-                    planes = work.tile([P, PACK, P], BF16, name="planes", tag="planes")
+                    planes = work.tile([P, 2, P, 2], BF16, name="planes", tag="planes")
                     for t in range(PACK):
                         nc.scalar.activation(
-                            out=planes[:, t, :],
+                            out=planes[:, t // 2, :, t % 2],
                             in_=bank[:, gl, t // 2, :].bitcast(BF16).rearrange("p (r e) -> p r e", e=2)[:, :, t % 2],
                             func=ACT.Copy,
                             scale=scale_cols[:, g, t : t + 1],
                         )
-                    nc.scalar.copy(out=packed_vals[:, g], in_=planes[:].rearrange("p t r -> p r t"))
+                    nc.scalar.copy(
+                        out=packed_words[:, g],
+                        in_=planes[:].rearrange("p u r e -> p u (r e)").bitcast(F32).rearrange("p u r -> p r u"),
+                    )
             tiles[("w_packed", j)] = w_packed
 
         def quantise(j):

@@ -55,7 +55,7 @@ def tile_flashneoxattention_pa_kernel(
     with ExitStack() as ctx:
         const = ctx.enter_context(tc.tile_pool(name="const", bufs=1))
         byte_pool = ctx.enter_context(tc.tile_pool(name="byte_pool", bufs=TILES))
-        work = ctx.enter_context(tc.tile_pool(name="work", bufs=3))
+        work = ctx.enter_context(tc.tile_pool(name="work", bufs=4))
         ps_words = ctx.enter_context(tc.psum_pool(name="ps_words", bufs=4))
         ps_sums = ctx.enter_context(tc.psum_pool(name="ps_sums", bufs=2))
         ps_done = ctx.enter_context(tc.psum_pool(name="ps_done", bufs=2))
@@ -297,25 +297,25 @@ def tile_flashneoxattention_pa_kernel(
         def at(n):
             return ORDER[n] if 0 <= n < TILES else None
 
-        for i in range(TILES + 5):
+        for i in range(TILES + 6):
             if at(i) is not None:
                 scale_product(at(i))
             if i == TILES:
                 turn(at(i - 1))
-            if at(i - 3) is not None:
-                multiply(at(i - 3), 0)
+            if at(i - 4) is not None:
+                multiply(at(i - 4), 0)
             if at(i - 1) is not None and i != TILES:
                 turn(at(i - 1))
             if i == 1:
                 turn_tokens()
                 make_tables()
-            if at(i - 3) is not None:
-                multiply(at(i - 3), 1)
             if at(i - 4) is not None:
-                rope_products(at(i - 4))
+                multiply(at(i - 4), 1)
+            if at(i - 5) is not None:
+                rope_products(at(i - 5))
             if i == 2:
                 quantise_tokens()
-            if at(i - 2) is not None:
-                quantise(at(i - 2))
-            if at(i - 5) is not None:
-                finish(at(i - 5))
+            if at(i - 3) is not None:
+                quantise(at(i - 3))
+            if at(i - 6) is not None:
+                finish(at(i - 6))

@@ -42,7 +42,7 @@ def has_rope(j):
 
 def scalar_passes(j):
     if has_rope(j):
-        return 1 if j % 4 != 3 else 0
+        return 1 if j % 4 != 0 else 0
     return 1 if j % 2 == 1 else 0
 
 
@@ -101,8 +101,8 @@ def tile_flashneoxattention_pa_kernel(
         nc.vector.tensor_copy(out=swap_halves[:, 0:HALF], in_=ident[:, HALF:P])
         nc.vector.tensor_copy(out=swap_halves[:, HALF:P], in_=ident[:, 0:HALF])
 
-        x_codes = const.tile([P, PASSES * N_MOVING], U32, name="x_codes", align_bytes=64)
-        x_scales = const.tile([P, PASSES * N_MOVING], U8, name="x_scales", align_bytes=64)
+        x_codes = const.tile([P, (PASSES + 1) * TOKENS], U32, name="x_codes", align_bytes=64)
+        x_scales = const.tile([P, (PASSES + 1) * TOKENS], U8, name="x_scales", align_bytes=64)
         x_packed = const.tile([P, PASSES, TOKENS * PACK], BF16, name="x_packed", align_bytes=64)
         bias = const.tile([P, TILES], F32, name="bias")
         tables = const.tile([P, COPIES, TOKENS], F32, name="tables")
@@ -184,7 +184,7 @@ def tile_flashneoxattention_pa_kernel(
             sums = tiles[("sums", j)]
             for g in (2 * half, 2 * half + 1):
                 rows = slice(g * P, (g + 1) * P)
-                toks = slice(g * N_MOVING, (g + 1) * N_MOVING)
+                toks = slice(g * TOKENS, g * TOKENS + N_MOVING)
                 nc.tensor.matmul_mx(
                     out=sums[:],
                     lhsT=w_codes[:, rows].bitcast(FP8X4),
@@ -205,10 +205,10 @@ def tile_flashneoxattention_pa_kernel(
             if has_rope(j):
                 products = work.tile([P, COPIES, TOKENS], F32, name="products", tag="products")
                 nc.vector.scalar_tensor_tensor(
-                    out=products[:].rearrange("p c n -> p (c n)"),
-                    in0=tiles[("sums", j)][:],
+                    out=products[:],
+                    in0=tiles[("sums", j)][:, 0:TOKENS].unsqueeze(1).to_broadcast([P, COPIES, TOKENS]),
                     scalar=bias[:, j : j + 1],
-                    in1=tables[:].rearrange("p c n -> p (c n)"),
+                    in1=tables[:],
                     op0=ALU.add,
                     op1=ALU.mult,
                 )
@@ -273,10 +273,10 @@ def tile_flashneoxattention_pa_kernel(
                 )
 
         def quantise_tokens():
-            for block in range(PASSES * COPIES):
+            for block in range(PASSES + 1):
                 cols = slice(block * TOKENS, (block + 1) * TOKENS)
                 nc.vector.quantize_mx(
-                    out=x_codes[:, cols].bitcast(FP8X4), scales=x_scales[:, cols], in_=x_packed[:, block // COPIES, :]
+                    out=x_codes[:, cols].bitcast(FP8X4), scales=x_scales[:, cols], in_=x_packed[:, block % PASSES, :]
                 )
 
         def make_tables():

@@ -42,7 +42,7 @@ def has_rope(j):
 
 def scalar_passes(j):
     if has_rope(j):
-        return 1 if j % 4 != 0 else 0
+        return 1 if j % 8 != 0 else 0
     return 1 if j % 2 == 1 else 0
 
 

@@ -68,7 +68,12 @@ def tile_flashneoxattention_pa_kernel(
             nc.scalar.dma_start(out=scale_rows[:, cols], in_=scale_vec[cols].partition_broadcast(P))
 
         scale_cols = const.tile([P, PASSES, PACK], F32, name="scale_cols")
-        nc.scalar.dma_start(out=scale_cols[:], in_=w_qkv_scale.rearrange("o (g p t) -> p (o g) t", p=P, t=PACK))
+
+        bias_rows = const.tile([P, P], BF16, name="bias_rows")
+        nc.vector.memset(bias_rows[:], 0.0)
+        trig = const.tile([P, 2, 4, HALF], BF16, name="trig")
+        cos_view = cos.rearrange("(a p) d -> p a d", p=P)
+        sin_view = sin.rearrange("(a p) d -> p a d", p=P)
 
         w_bytes = {}
         for j in ORDER:
@@ -80,18 +85,14 @@ def tile_flashneoxattention_pa_kernel(
             if n == 2:
                 nc.sync.dma_start(out=x_rows[:], in_=hidden_states.rearrange("(a p) k -> p a k", p=P))
             nc.sync.dma_start(out=w_bytes[j][:], in_=w_qkv_bytes[j * P : (j + 1) * P, :])
+            if n == 2:
+                nc.sync.dma_start(out=scale_cols[:], in_=w_qkv_scale.rearrange("o (g p t) -> p (o g) t", p=P, t=PACK))
+                nc.sync.dma_start(out=bias_rows[0:TILES, :], in_=b_qkv.rearrange("(j p) -> j p", p=P))
+                nc.sync.dma_start(out=trig[:, :, 0, :], in_=cos_view)
+                nc.sync.dma_start(out=trig[:, :, 1, :], in_=cos_view)
+                nc.sync.dma_start(out=trig[:, :, 2, :], in_=sin_view)
+                nc.sync.dma_start(out=trig[:, :, 3, :], in_=sin_view)
 
-        bias_rows = const.tile([P, P], BF16, name="bias_rows")
-        nc.vector.memset(bias_rows[:], 0.0)
-        nc.scalar.dma_start(out=bias_rows[0:TILES, :], in_=b_qkv.rearrange("(j p) -> j p", p=P))
-
-        trig = const.tile([P, 2, 4, HALF], BF16, name="trig")
-        cos_view = cos.rearrange("(a p) d -> p a d", p=P)
-        sin_view = sin.rearrange("(a p) d -> p a d", p=P)
-        nc.scalar.dma_start(out=trig[:, :, 0, :], in_=cos_view)
-        nc.scalar.dma_start(out=trig[:, :, 1, :], in_=cos_view)
-        nc.scalar.dma_start(out=trig[:, :, 2, :], in_=sin_view)
-        nc.scalar.dma_start(out=trig[:, :, 3, :], in_=sin_view)
 
         ident = const.tile([P, P], F32, name="ident")
         make_identity(nc, ident[:])
@@ -214,10 +215,10 @@ def tile_flashneoxattention_pa_kernel(
                 )
                 tiles[("products", j)] = products
 
-        def store_group(j, a, staged):
-            first_head = (j % HEADS) - (GROUP - 1)
-            nc.sync.dma_start(
-                out=outs[j // HEADS][a * P : (a + 1) * P, first_head : first_head + GROUP, :].rearrange(
+        def store_heads(queue, j, count, a, staged):
+            first_head = (j % HEADS) - (count - 1)
+            queue.dma_start(
+                out=outs[j // HEADS][a * P : (a + 1) * P, first_head : first_head + count, :].rearrange(
                     "t h d -> t (h d)"
                 ),
                 in_=staged[:],
@@ -246,19 +247,21 @@ def tile_flashneoxattention_pa_kernel(
             ready = (GROUP - 1) * D
             if j == LAST - 1:
                 for a in range(2):
-                    early = work.tile([P, GROUP * D], F32, name="early", tag="staged")
-                    nc.scalar.copy(out=early[:, 0:ready], in_=done[a][:, 0:ready])
-                    tiles[("staged", a)] = early
+                    early = work.tile([P, ready], F32, name="early", tag="staged")
+                    nc.scalar.copy(out=early[:], in_=done[a][:, 0:ready])
+                    store_heads(nc.sync, j, GROUP - 1, a, early)
             if j == LAST:
-                nc.scalar.copy(out=tiles[("staged", 0)][:, ready : GROUP * D], in_=done[0][:, ready : GROUP * D])
-                store_group(j, 0, tiles[("staged", 0)])
-                nc.vector.tensor_copy(out=tiles[("staged", 1)][:, ready : GROUP * D], in_=done[1][:, ready : GROUP * D])
-                store_group(j, 1, tiles[("staged", 1)])
+                last_0 = work.tile([P, D], F32, name="last_0", tag="last")
+                nc.scalar.copy(out=last_0[:], in_=done[0][:, ready : GROUP * D])
+                store_heads(nc.sync, j, 1, 0, last_0)
+                last_1 = work.tile([P, D], F32, name="last_1", tag="last")
+                nc.vector.tensor_copy(out=last_1[:], in_=done[1][:, ready : GROUP * D])
+                store_heads(nc.scalar, j, 1, 1, last_1)
             elif place == GROUP - 1:
                 for a in range(2):
                     staged = work.tile([P, GROUP * D], F32, name="staged", tag="staged")
                     nc.scalar.copy(out=staged[:], in_=done[a][:])
-                    store_group(j, a, staged)
+                    store_heads(nc.sync, j, GROUP, a, staged)
 
         def turn_tokens():
             for g in range(PASSES):

@@ -27,23 +27,27 @@ K_PASS = P * PACK
 PASSES = HID // K_PASS
 WORDS_PASS = K_PASS // 2
 GROUP = 4
-
+TOKEN_TILES = TOKENS // P
 COPIES = 2
 N_MOVING = COPIES * TOKENS
+GP_PASS = PASSES - 1
 
-ORDER = list(range(2 * HEADS, TILES)) + list(range(2 * HEADS))
-FIRST = ORDER[0]
+ORDER = [j for pair in range(HEADS) for j in (2 * pair, 2 * pair + 1, 2 * HEADS + pair)]
 LAST = ORDER[TILES - 1]
+LAST_ROPE = ORDER[TILES - 2]
+EARLY = 2
+
+LAG_SCALE = 1
+LAG_TURN = 2
+LAG_EVAC = 3
+LAG_QUANT = 4
+LAG_MUL = 5
+LAG_ROPE = 6
+LAG_FIN = 7
 
 
 def has_rope(j):
     return j < 2 * HEADS
-
-
-def scalar_passes(j):
-    if has_rope(j):
-        return 1 if j % 8 != 0 else 0
-    return 1 if j % 2 == 1 else 0
 
 
 def tile_flashneoxattention_pa_kernel(
@@ -56,6 +60,7 @@ def tile_flashneoxattention_pa_kernel(
         const = ctx.enter_context(tc.tile_pool(name="const", bufs=1))
         byte_pool = ctx.enter_context(tc.tile_pool(name="byte_pool", bufs=TILES))
         work = ctx.enter_context(tc.tile_pool(name="work", bufs=4))
+        v_pool = ctx.enter_context(tc.tile_pool(name="v_pool", bufs=2))
         ps_words = ctx.enter_context(tc.psum_pool(name="ps_words", bufs=4))
         ps_sums = ctx.enter_context(tc.psum_pool(name="ps_sums", bufs=2))
         ps_done = ctx.enter_context(tc.psum_pool(name="ps_done", bufs=2))
@@ -68,9 +73,9 @@ def tile_flashneoxattention_pa_kernel(
             nc.scalar.dma_start(out=scale_rows[:, cols], in_=scale_vec[cols].partition_broadcast(P))
 
         scale_cols = const.tile([P, PASSES, PACK], F32, name="scale_cols")
-
         bias_rows = const.tile([P, P], BF16, name="bias_rows")
         nc.vector.memset(bias_rows[:], 0.0)
+        bias_v = const.tile([P, HEADS * D], BF16, name="bias_v")
         trig = const.tile([P, 2, 4, HALF], BF16, name="trig")
         cos_view = cos.rearrange("(a p) d -> p a d", p=P)
         sin_view = sin.rearrange("(a p) d -> p a d", p=P)
@@ -92,7 +97,8 @@ def tile_flashneoxattention_pa_kernel(
                 nc.sync.dma_start(out=trig[:, :, 1, :], in_=cos_view)
                 nc.sync.dma_start(out=trig[:, :, 2, :], in_=sin_view)
                 nc.sync.dma_start(out=trig[:, :, 3, :], in_=sin_view)
-
+            if n == 5:
+                nc.sync.dma_start(out=bias_v[:], in_=b_qkv[2 * HEADS * D : 3 * HEADS * D].partition_broadcast(P))
 
         ident = const.tile([P, P], F32, name="ident")
         make_identity(nc, ident[:])
@@ -110,71 +116,77 @@ def tile_flashneoxattention_pa_kernel(
 
         tiles = {}
 
-        def scale_product(j):
+        def on_bytes(j):
+            return j in ORDER[0:EARLY]
+
+        def widen(j):
             w_rows = work.tile([P, HID], BF16, name="w_rows", tag="w_rows")
-            split = (PASSES - scalar_passes(j)) * K_PASS
-            if split < HID:
-                nc.scalar.copy(out=w_rows[:, split:HID], in_=w_bytes[j][:, split:HID].bitcast(FP8))
-            pieces = 1
-            if j == FIRST:
-                pieces = split // K_PASS
-            if j == LAST:
-                pieces = 2
-            width = split // pieces
-            for c in range(pieces):
-                cols = slice(c * width, (c + 1) * width)
-                nc.vector.tensor_tensor(
-                    out=w_rows[:, cols], in0=w_bytes[j][:, cols].bitcast(FP8), in1=scale_rows[:, cols], op=ALU.mult
-                )
+            if on_bytes(j):
+                pieces = PASSES if j == ORDER[0] else 1
+                width = HID // pieces
+                for c in range(pieces):
+                    cols = slice(c * width, (c + 1) * width)
+                    nc.vector.tensor_tensor(
+                        out=w_rows[:, cols], in0=w_bytes[j][:, cols].bitcast(FP8), in1=scale_rows[:, cols], op=ALU.mult
+                    )
+            else:
+                nc.scalar.copy(out=w_rows[:], in_=w_bytes[j][:].bitcast(FP8))
             tiles[("w_rows", j)] = w_rows
+
+        def scale_on_gpsimd(j):
+            if not on_bytes(j):
+                w_rows = tiles[("w_rows", j)]
+                cols = slice(GP_PASS * K_PASS, (GP_PASS + 1) * K_PASS)
+                nc.gpsimd.tensor_tensor(
+                    out=w_rows[:, cols], in0=w_rows[:, cols], in1=scale_rows[:, cols], op=ALU.mult
+                )
 
         def transpose_pass(dst, words, g, u):
             nc.tensor.transpose(dst, words[:, WORDS_PASS * g + u : WORDS_PASS * (g + 1) : 2], ident[:])
 
         def turn(j):
             words = tiles[("w_rows", j)][:].bitcast(F32)
-            w_packed = work.tile([P, PASSES * P * PACK], BF16, name="w_packed", tag="w_packed", align_bytes=64)
-            packed_words = w_packed[:].bitcast(F32).rearrange("p (g r u) -> p g r u", g=PASSES, u=2)
-            packed_vals = w_packed[:].rearrange("p (g r t) -> p g r t", g=PASSES, t=PACK)
+            banks = []
             for b in range(2):
                 bank = ps_words.tile([P, 2, 2, P], F32, name="bank", tag="words")
                 for gl in range(2):
                     for u in range(2):
-                        transpose_pass(bank[:, gl, u, :], words, 2 * b + gl, u)
-                scaled = max(0, min(2, PASSES - scalar_passes(j) - 2 * b))
-                if scaled > 0:
+                        transpose_pass(bank[:, u, gl, :], words, 2 * b + gl, u)
+                banks.append(bank)
+            tiles[("banks", j)] = banks
+
+        def scale_on_vector(packed, bank, g, gl, count):
+            vals = bank[:, :, gl : gl + count, :].bitcast(BF16).rearrange("p u g (r e) -> p g r u e", e=2)
+            scales = (
+                scale_cols[:, g : g + count, :]
+                .rearrange("p g (u e) -> p g u e", e=2)
+                .unsqueeze(2)
+                .to_broadcast([P, count, P, 2, 2])
+            )
+            nc.vector.tensor_tensor(out=packed[:, g : g + count], in0=vals, in1=scales, op=ALU.mult)
+
+        def empty(j):
+            w_packed = work.tile([P, PASSES * P * PACK], BF16, name="w_packed", tag="w_packed", align_bytes=64)
+            packed_words = w_packed[:].bitcast(F32).rearrange("p (g r u) -> p g r u", g=PASSES, u=2)
+            packed_vals = w_packed[:].rearrange("p (g r u e) -> p g r u e", g=PASSES, u=2, e=2)
+            banks = tiles[("banks", j)]
+            if on_bytes(j):
+                for b in range(2):
                     nc.scalar.copy(
-                        out=packed_words[:, 2 * b : 2 * b + scaled],
-                        in_=bank[:, 0:scaled].rearrange("p g u r -> p g r u"),
+                        out=packed_words[:, 2 * b : 2 * b + 2], in_=banks[b][:].rearrange("p u g r -> p g r u")
                     )
-                for gl in range(scaled, 2):
-                    g = 2 * b + gl
-                    planes = work.tile([P, 2, P, 2], BF16, name="planes", tag="planes")
-                    for t in range(PACK):
-                        nc.scalar.activation(
-                            out=planes[:, t // 2, :, t % 2],
-                            in_=bank[:, gl, t // 2, :].bitcast(BF16).rearrange("p (r e) -> p r e", e=2)[:, :, t % 2],
-                            func=ACT.Copy,
-                            scale=scale_cols[:, g, t : t + 1],
-                        )
-                    nc.scalar.copy(
-                        out=packed_words[:, g],
-                        in_=planes[:].rearrange("p u r e -> p u (r e)").bitcast(F32).rearrange("p u r -> p r u"),
-                    )
+            else:
+                scale_on_vector(packed_vals, banks[1], 2, 0, 1)
+                scale_on_vector(packed_vals, banks[0], 0, 0, 2)
+                nc.scalar.copy(out=packed_words[:, GP_PASS], in_=banks[1][:, :, 1, :].rearrange("p u r -> p r u"))
             tiles[("w_packed", j)] = w_packed
 
         def quantise(j):
             w_codes = work.tile([P, PASSES * P], U32, name="w_codes", tag="w_codes", align_bytes=64)
             w_scales = work.tile([P, PASSES * P], U8, name="w_scales", tag="w_scales", align_bytes=64)
-            pieces = 2 if j == LAST else 1
-            width = PASSES * P // pieces
-            for c in range(pieces):
-                cols = slice(c * width, (c + 1) * width)
-                nc.vector.quantize_mx(
-                    out=w_codes[:, cols].bitcast(FP8X4),
-                    scales=w_scales[:, cols],
-                    in_=tiles[("w_packed", j)][:, PACK * c * width : PACK * (c + 1) * width],
-                )
+            nc.vector.quantize_mx(
+                out=w_codes[:].bitcast(FP8X4), scales=w_scales[:], in_=tiles[("w_packed", j)][:]
+            )
             tiles[("w_codes", j)] = (w_codes, w_scales)
 
         def multiply(j, half):
@@ -183,37 +195,32 @@ def tile_flashneoxattention_pa_kernel(
                 new_sums = ps_sums.tile([P, N_MOVING], F32, name="new_sums", tag="sums")
                 tiles[("sums", j)] = new_sums
             sums = tiles[("sums", j)]
-            for g in (2 * half, 2 * half + 1):
-                rows = slice(g * P, (g + 1) * P)
-                toks = slice(g * TOKENS, g * TOKENS + N_MOVING)
-                nc.tensor.matmul_mx(
-                    out=sums[:],
-                    lhsT=w_codes[:, rows].bitcast(FP8X4),
-                    lhsT_scale=w_scales[:, rows],
-                    rhs=x_codes[:, toks].bitcast(FP8X4),
-                    rhs_scale=x_scales[:, toks],
-                    start=(g == 0),
-                    stop=(g == PASSES - 1),
-                )
-            if half == 1 and not has_rope(j):
-                v_head = work.tile([P, TOKENS], F32, name="v_head", tag="v_head")
-                nc.scalar.activation(
-                    out=v_head[:], in_=sums[:, 0:TOKENS], func=ACT.Identity, bias=bias[:, j : j + 1], scale=1.0
-                )
-                tiles[("v_head", j)] = v_head
-
-        def rope_products(j):
             if has_rope(j):
-                products = work.tile([P, COPIES, TOKENS], F32, name="products", tag="products")
-                nc.vector.scalar_tensor_tensor(
-                    out=products[:],
-                    in0=tiles[("sums", j)][:, 0:TOKENS].unsqueeze(1).to_broadcast([P, COPIES, TOKENS]),
-                    scalar=bias[:, j : j + 1],
-                    in1=tables[:],
-                    op0=ALU.add,
-                    op1=ALU.mult,
-                )
-                tiles[("products", j)] = products
+                for g in (2 * half, 2 * half + 1):
+                    rows = slice(g * P, (g + 1) * P)
+                    toks = slice(g * TOKENS, g * TOKENS + N_MOVING)
+                    nc.tensor.matmul_mx(
+                        out=sums[:],
+                        lhsT=w_codes[:, rows].bitcast(FP8X4),
+                        lhsT_scale=w_scales[:, rows],
+                        rhs=x_codes[:, toks].bitcast(FP8X4),
+                        rhs_scale=x_scales[:, toks],
+                        start=(g == 0),
+                        stop=(g == PASSES - 1),
+                    )
+            else:
+                for g in range(PASSES):
+                    rows = slice(g * P, (g + 1) * P)
+                    toks = slice(g * TOKENS + half * P, g * TOKENS + (half + 1) * P)
+                    nc.tensor.matmul_mx(
+                        out=sums[:, half * D : (half + 1) * D],
+                        lhsT=x_codes[:, toks].bitcast(FP8X4),
+                        lhsT_scale=x_scales[:, toks],
+                        rhs=w_codes[:, rows].bitcast(FP8X4),
+                        rhs_scale=w_scales[:, rows],
+                        start=(g == 0),
+                        stop=(g == PASSES - 1),
+                    )
 
         def store_heads(queue, j, count, a, staged):
             first_head = (j % HEADS) - (count - 1)
@@ -221,47 +228,73 @@ def tile_flashneoxattention_pa_kernel(
                 out=outs[j // HEADS][a * P : (a + 1) * P, first_head : first_head + count, :].rearrange(
                     "t h d -> t (h d)"
                 ),
-                in_=staged[:],
+                in_=staged,
             )
 
+        def rope_or_bias(j):
+            sums = tiles[("sums", j)]
+            if has_rope(j):
+                products = work.tile([P, COPIES, TOKENS], F32, name="products", tag="products")
+                nc.vector.scalar_tensor_tensor(
+                    out=products[:],
+                    in0=sums[:, 0:TOKENS].unsqueeze(1).to_broadcast([P, COPIES, TOKENS]),
+                    scalar=bias[:, j : j + 1],
+                    in1=tables[:],
+                    op0=ALU.add,
+                    op1=ALU.mult,
+                )
+                tiles[("products", j)] = products
+            else:
+                h = j - 2 * HEADS
+                place = j % GROUP
+                if place == 0:
+                    new_stage = v_pool.tile([P, TOKEN_TILES, GROUP * D], F32, name="new_stage", tag="v_stage")
+                    tiles["v_stage"] = new_stage
+                stage = tiles["v_stage"]
+                cols = slice(place * D, (place + 1) * D)
+                nc.vector.tensor_tensor(
+                    out=stage[:, :, cols],
+                    in0=sums[:, 0:TOKENS].rearrange("p (a d) -> p a d", a=TOKEN_TILES),
+                    in1=bias_v[:, h * D : (h + 1) * D].unsqueeze(1).to_broadcast([P, TOKEN_TILES, D]),
+                    op=ALU.add,
+                )
+                if j == LAST - 1:
+                    for a in range(TOKEN_TILES):
+                        store_heads(nc.sync, j, GROUP - 1, a, stage[:, a, 0 : (GROUP - 1) * D])
+                elif j == LAST:
+                    store_heads(nc.sync, j, 1, 0, stage[:, 0, cols])
+                    store_heads(nc.scalar, j, 1, 1, stage[:, 1, cols])
+                elif place == GROUP - 1:
+                    for a in range(TOKEN_TILES):
+                        store_heads(nc.sync, j, GROUP, a, stage[:, a, :])
+
         def finish(j):
+            if not has_rope(j):
+                return
             place = j % GROUP
             if place == 0:
                 done_0 = ps_done.tile([P, GROUP * D], F32, name="done_0", tag="done")
                 done_1 = ps_done.tile([P, GROUP * D], F32, name="done_1", tag="done")
                 tiles["done"] = (done_0, done_1)
             done = tiles["done"]
-            for a in range(2):
+            products = tiles[("products", j)]
+            for a in range(TOKEN_TILES):
                 dst = done[a][:, place * D : (place + 1) * D]
                 toks = slice(a * P, (a + 1) * P)
-                if has_rope(j):
-                    products = tiles[("products", j)]
-                    nc.tensor.matmul(
-                        dst, lhsT=products[:, 0, toks], rhs=ident[:], is_transpose=True, start=True, stop=False
-                    )
-                    nc.tensor.matmul(
-                        dst, lhsT=products[:, 1, toks], rhs=swap_halves[:], is_transpose=True, start=False, stop=True
-                    )
-                else:
-                    nc.tensor.transpose(dst, tiles[("v_head", j)][:, toks], ident[:])
-            ready = (GROUP - 1) * D
-            if j == LAST - 1:
-                for a in range(2):
-                    early = work.tile([P, ready], F32, name="early", tag="staged")
-                    nc.scalar.copy(out=early[:], in_=done[a][:, 0:ready])
-                    store_heads(nc.sync, j, GROUP - 1, a, early)
-            if j == LAST:
-                last_0 = work.tile([P, D], F32, name="last_0", tag="last")
-                nc.scalar.copy(out=last_0[:], in_=done[0][:, ready : GROUP * D])
-                store_heads(nc.sync, j, 1, 0, last_0)
-                last_1 = work.tile([P, D], F32, name="last_1", tag="last")
-                nc.vector.tensor_copy(out=last_1[:], in_=done[1][:, ready : GROUP * D])
-                store_heads(nc.scalar, j, 1, 1, last_1)
-            elif place == GROUP - 1:
-                for a in range(2):
+                nc.tensor.matmul(
+                    dst, lhsT=products[:, 0, toks], rhs=ident[:], is_transpose=True, start=True, stop=False
+                )
+                nc.tensor.matmul(
+                    dst, lhsT=products[:, 1, toks], rhs=swap_halves[:], is_transpose=True, start=False, stop=True
+                )
+            if place == GROUP - 1:
+                for a in range(TOKEN_TILES):
                     staged = work.tile([P, GROUP * D], F32, name="staged", tag="staged")
-                    nc.scalar.copy(out=staged[:], in_=done[a][:])
-                    store_heads(nc.sync, j, GROUP, a, staged)
+                    if j == LAST_ROPE and a == 1:
+                        nc.vector.tensor_copy(out=staged[:], in_=done[a][:])
+                    else:
+                        nc.scalar.copy(out=staged[:], in_=done[a][:])
+                    store_heads(nc.sync, j, GROUP, a, staged[:])
 
         def turn_tokens():
             for g in range(PASSES):
@@ -300,25 +333,28 @@ def tile_flashneoxattention_pa_kernel(
         def at(n):
             return ORDER[n] if 0 <= n < TILES else None
 
-        for i in range(TILES + 6):
+        for i in range(TILES + LAG_FIN):
             if at(i) is not None:
-                scale_product(at(i))
-            if i == TILES:
-                turn(at(i - 1))
-            if at(i - 4) is not None:
-                multiply(at(i - 4), 0)
-            if at(i - 1) is not None and i != TILES:
-                turn(at(i - 1))
+                widen(at(i))
+            if at(i - LAG_SCALE) is not None:
+                scale_on_gpsimd(at(i - LAG_SCALE))
+            if at(i - LAG_EVAC) is not None:
+                empty(at(i - LAG_EVAC))
+            if at(i - LAG_MUL) is not None:
+                multiply(at(i - LAG_MUL), 0)
             if i == 1:
                 turn_tokens()
+            if i == 3:
                 make_tables()
-            if at(i - 4) is not None:
-                multiply(at(i - 4), 1)
-            if at(i - 5) is not None:
-                rope_products(at(i - 5))
-            if i == 2:
+            if at(i - LAG_TURN) is not None:
+                turn(at(i - LAG_TURN))
+            if at(i - LAG_MUL) is not None:
+                multiply(at(i - LAG_MUL), 1)
+            if at(i - LAG_ROPE) is not None:
+                rope_or_bias(at(i - LAG_ROPE))
+            if i == LAG_QUANT:
                 quantise_tokens()
-            if at(i - 3) is not None:
-                quantise(at(i - 3))
-            if at(i - 6) is not None:
-                finish(at(i - 6))
+            if at(i - LAG_QUANT) is not None:
+                quantise(at(i - LAG_QUANT))
+            if at(i - LAG_FIN) is not None:
+                finish(at(i - LAG_FIN))

@@ -33,9 +33,10 @@ N_MOVING = COPIES * TOKENS
 GP_PASS = PASSES - 1
 
 ORDER = [j for pair in range(HEADS) for j in (2 * pair, 2 * pair + 1, 2 * HEADS + pair)]
+ORDER = ORDER[0 : TILES - 4] + ORDER[TILES - 3 : TILES - 1] + [ORDER[TILES - 4], ORDER[TILES - 1]]
 LAST = ORDER[TILES - 1]
-LAST_ROPE = ORDER[TILES - 2]
-EARLY = 2
+LAST_ROPE = ORDER[TILES - 3]
+EARLY = 4
 
 LAG_SCALE = 1
 LAG_TURN = 2
@@ -307,6 +308,7 @@ def tile_flashneoxattention_pa_kernel(
                     out=x_packed[:, g, :].bitcast(F32).rearrange("p (r u) -> p r u", u=2),
                     in_=bank[:].rearrange("p u r -> p r u"),
                 )
+            nc.scalar.activation(out=trig[:, :, 3, :], in_=trig[:, :, 3, :], func=ACT.Copy, scale=-1.0)
 
         def quantise_tokens():
             for block in range(PASSES + 1):
@@ -319,7 +321,6 @@ def tile_flashneoxattention_pa_kernel(
             bias_bank = ps_words.tile([P, P], BF16, name="bias_bank", tag="words")
             nc.tensor.transpose(bias_bank[:], bias_rows[:], ident_bf[:])
             nc.scalar.copy(out=bias[:], in_=bias_bank[:, 0:TILES])
-            nc.scalar.activation(out=trig[:, :, 3, :], in_=trig[:, :, 3, :], func=ACT.Copy, scale=-1.0)
             trig_bank = ps_words.tile([P, COPIES, TOKENS], BF16, name="trig_bank", tag="words")
             for c in range(COPIES):
                 for a in range(2):
@@ -356,5 +357,7 @@ def tile_flashneoxattention_pa_kernel(
                 quantise_tokens()
             if at(i - LAG_QUANT) is not None:
                 quantise(at(i - LAG_QUANT))
+                if at(i) is not None and not on_bytes(at(i)):
+                    nc.gpsimd.memset(tiles[("w_packed", at(i - LAG_QUANT))][:, 0:2], 0.0)
             if at(i - LAG_FIN) is not None:
                 finish(at(i - LAG_FIN))

@@ -166,6 +166,24 @@ def tile_flashneoxattention_pa_kernel(
             )
             nc.vector.tensor_tensor(out=packed[:, g : g + count], in0=vals, in1=scales, op=ALU.mult)
 
+        def on_scalar(j):
+            n = ORDER.index(j)
+            return n >= EARLY and n % 2 == 0
+
+        def scale_on_scalar(packed_words, bank, g, gl):
+            planes = work.tile([P, 2, P, 2], BF16, name="planes", tag="planes")
+            for t in range(PACK):
+                nc.scalar.activation(
+                    out=planes[:, t // 2, :, t % 2],
+                    in_=bank[:, t // 2, gl, :].bitcast(BF16).rearrange("p (r e) -> p r e", e=2)[:, :, t % 2],
+                    func=ACT.Copy,
+                    scale=scale_cols[:, g, t : t + 1],
+                )
+            nc.scalar.copy(
+                out=packed_words[:, g],
+                in_=planes[:].rearrange("p u r e -> p u (r e)").bitcast(F32).rearrange("p u r -> p r u"),
+            )
+
         def empty(j):
             w_packed = work.tile([P, PASSES * P * PACK], BF16, name="w_packed", tag="w_packed", align_bytes=64)
             packed_words = w_packed[:].bitcast(F32).rearrange("p (g r u) -> p g r u", g=PASSES, u=2)
@@ -177,7 +195,10 @@ def tile_flashneoxattention_pa_kernel(
                         out=packed_words[:, 2 * b : 2 * b + 2], in_=banks[b][:].rearrange("p u g r -> p g r u")
                     )
             else:
-                scale_on_vector(packed_vals, banks[1], 2, 0, 1)
+                if on_scalar(j):
+                    scale_on_scalar(packed_words, banks[1], 2, 0)
+                else:
+                    scale_on_vector(packed_vals, banks[1], 2, 0, 1)
                 scale_on_vector(packed_vals, banks[0], 0, 0, 2)
                 nc.scalar.copy(out=packed_words[:, GP_PASS], in_=banks[1][:, :, 1, :].rearrange("p u r -> p r u"))
             tiles[("w_packed", j)] = w_packed

@@ -35,16 +35,19 @@ GP_PASS = PASSES - 1
 ORDER = [j for pair in range(HEADS) for j in (2 * pair, 2 * pair + 1, 2 * HEADS + pair)]
 ORDER = ORDER[0 : TILES - 4] + ORDER[TILES - 3 : TILES - 1] + [ORDER[TILES - 4], ORDER[TILES - 1]]
 LAST = ORDER[TILES - 1]
-LAST_ROPE = ORDER[TILES - 3]
-EARLY = 4
+EARLY = 5
 
-LAG_SCALE = 1
-LAG_TURN = 2
-LAG_EVAC = 3
-LAG_QUANT = 4
-LAG_MUL = 5
-LAG_ROPE = 6
-LAG_FIN = 7
+TOK = 2
+TOKQ = 3
+TABLES = 3
+LAG_CAST = -2
+LAG_GP = 0
+LAG_TURN = 1
+LAG_EVAC = 2
+LAG_QUANT = 3
+LAG_MUL = 4
+LAG_ROPE = 5
+LAG_FIN = 6
 
 
 def has_rope(j):
@@ -61,7 +64,9 @@ def tile_flashneoxattention_pa_kernel(
         const = ctx.enter_context(tc.tile_pool(name="const", bufs=1))
         byte_pool = ctx.enter_context(tc.tile_pool(name="byte_pool", bufs=TILES))
         work = ctx.enter_context(tc.tile_pool(name="work", bufs=4))
+        rows_pool = ctx.enter_context(tc.tile_pool(name="rows_pool", bufs=6))
         v_pool = ctx.enter_context(tc.tile_pool(name="v_pool", bufs=2))
+        stage_pool = ctx.enter_context(tc.tile_pool(name="stage_pool", bufs=3))
         ps_words = ctx.enter_context(tc.psum_pool(name="ps_words", bufs=4))
         ps_sums = ctx.enter_context(tc.psum_pool(name="ps_sums", bufs=2))
         ps_done = ctx.enter_context(tc.psum_pool(name="ps_done", bufs=2))
@@ -88,7 +93,7 @@ def tile_flashneoxattention_pa_kernel(
         x_rows = const.tile([P, 2, HID], BF16, name="x_rows")
         for n in range(TILES):
             j = ORDER[n]
-            if n == 2:
+            if n == 3:
                 nc.sync.dma_start(out=x_rows[:], in_=hidden_states.rearrange("(a p) k -> p a k", p=P))
             nc.sync.dma_start(out=w_bytes[j][:], in_=w_qkv_bytes[j * P : (j + 1) * P, :])
             if n == 2:
@@ -121,15 +126,19 @@ def tile_flashneoxattention_pa_kernel(
             return j in ORDER[0:EARLY]
 
         def widen(j):
-            w_rows = work.tile([P, HID], BF16, name="w_rows", tag="w_rows")
+            w_rows = rows_pool.tile([P, HID], BF16, name="w_rows", tag="w_rows")
             if on_bytes(j):
-                pieces = PASSES if j == ORDER[0] else 1
-                width = HID // pieces
-                for c in range(pieces):
-                    cols = slice(c * width, (c + 1) * width)
-                    nc.vector.tensor_tensor(
-                        out=w_rows[:, cols], in0=w_bytes[j][:, cols].bitcast(FP8), in1=scale_rows[:, cols], op=ALU.mult
-                    )
+                if j == ORDER[0]:
+                    tiles["first"] = w_rows
+                elif j == ORDER[1]:
+                    for g in range(PASSES):
+                        cols = slice(g * K_PASS, (g + 1) * K_PASS)
+                        for jj, dst in ((ORDER[0], tiles["first"]), (j, w_rows)):
+                            nc.vector.tensor_tensor(
+                                out=dst[:, cols], in0=w_bytes[jj][:, cols].bitcast(FP8), in1=scale_rows[:, cols], op=ALU.mult
+                            )
+                else:
+                    nc.vector.tensor_tensor(out=w_rows[:], in0=w_bytes[j][:].bitcast(FP8), in1=scale_rows[:], op=ALU.mult)
             else:
                 nc.scalar.copy(out=w_rows[:], in_=w_bytes[j][:].bitcast(FP8))
             tiles[("w_rows", j)] = w_rows
@@ -138,9 +147,14 @@ def tile_flashneoxattention_pa_kernel(
             if not on_bytes(j):
                 w_rows = tiles[("w_rows", j)]
                 cols = slice(GP_PASS * K_PASS, (GP_PASS + 1) * K_PASS)
+                w_gp = work.tile([P, K_PASS], BF16, name="w_gp", tag="w_gp")
                 nc.gpsimd.tensor_tensor(
-                    out=w_rows[:, cols], in0=w_rows[:, cols], in1=scale_rows[:, cols], op=ALU.mult
+                    out=w_gp[:].rearrange("p (u m e) -> p u m e", u=2, e=2),
+                    in0=w_rows[:, cols].rearrange("p (m u e) -> p u m e", u=2, e=2),
+                    in1=scale_rows[:, cols].rearrange("p (m u e) -> p u m e", u=2, e=2),
+                    op=ALU.mult,
                 )
+                tiles[("w_gp", j)] = w_gp
 
         def transpose_pass(dst, words, g, u):
             nc.tensor.transpose(dst, words[:, WORDS_PASS * g + u : WORDS_PASS * (g + 1) : 2], ident[:])
@@ -152,7 +166,12 @@ def tile_flashneoxattention_pa_kernel(
                 bank = ps_words.tile([P, 2, 2, P], F32, name="bank", tag="words")
                 for gl in range(2):
                     for u in range(2):
-                        transpose_pass(bank[:, u, gl, :], words, 2 * b + gl, u)
+                        g = 2 * b + gl
+                        if g == GP_PASS and not on_bytes(j):
+                            halves = tiles[("w_gp", j)][:].bitcast(F32)
+                            nc.tensor.transpose(bank[:, u, gl, :], halves[:, u * P : (u + 1) * P], ident[:])
+                        else:
+                            transpose_pass(bank[:, u, gl, :], words, g, u)
                 banks.append(bank)
             tiles[("banks", j)] = banks
 
@@ -168,7 +187,7 @@ def tile_flashneoxattention_pa_kernel(
 
         def on_scalar(j):
             n = ORDER.index(j)
-            return n >= EARLY and n % 2 == 0
+            return n >= EARLY and has_rope(j)
 
         def scale_on_scalar(packed_words, bank, g, gl):
             planes = work.tile([P, 2, P, 2], BF16, name="planes", tag="planes")
@@ -295,28 +314,35 @@ def tile_flashneoxattention_pa_kernel(
                 return
             place = j % GROUP
             if place == 0:
-                done_0 = ps_done.tile([P, GROUP * D], F32, name="done_0", tag="done")
-                done_1 = ps_done.tile([P, GROUP * D], F32, name="done_1", tag="done")
-                tiles["done"] = (done_0, done_1)
-            done = tiles["done"]
+                new_stage = stage_pool.tile([P, TOKEN_TILES, GROUP * D], F32, name="new_stage", tag="rope_stage")
+                tiles["rope_stage"] = new_stage
+            stage = tiles["rope_stage"]
+            done = ps_done.tile([P, TOKEN_TILES, D], F32, name="done", tag="done")
             products = tiles[("products", j)]
             for a in range(TOKEN_TILES):
-                dst = done[a][:, place * D : (place + 1) * D]
                 toks = slice(a * P, (a + 1) * P)
                 nc.tensor.matmul(
-                    dst, lhsT=products[:, 0, toks], rhs=ident[:], is_transpose=True, start=True, stop=False
+                    done[:, a, :], lhsT=products[:, 0, toks], rhs=ident[:], is_transpose=True, start=True, stop=False
                 )
                 nc.tensor.matmul(
-                    dst, lhsT=products[:, 1, toks], rhs=swap_halves[:], is_transpose=True, start=False, stop=True
+                    done[:, a, :],
+                    lhsT=products[:, 1, toks],
+                    rhs=swap_halves[:],
+                    is_transpose=True,
+                    start=False,
+                    stop=True,
                 )
+            tiles[("done", j)] = (done, stage)
+
+        def copy_out(j):
+            if not has_rope(j):
+                return
+            done, stage = tiles[("done", j)]
+            place = j % GROUP
+            nc.scalar.copy(out=stage[:, :, place * D : (place + 1) * D], in_=done[:])
             if place == GROUP - 1:
                 for a in range(TOKEN_TILES):
-                    staged = work.tile([P, GROUP * D], F32, name="staged", tag="staged")
-                    if j == LAST_ROPE and a == 1:
-                        nc.vector.tensor_copy(out=staged[:], in_=done[a][:])
-                    else:
-                        nc.scalar.copy(out=staged[:], in_=done[a][:])
-                    store_heads(nc.sync, j, GROUP, a, staged[:])
+                    store_heads(nc.sync, j, GROUP, a, stage[:, a, :])
 
         def turn_tokens():
             for g in range(PASSES):
@@ -356,29 +382,33 @@ def tile_flashneoxattention_pa_kernel(
             return ORDER[n] if 0 <= n < TILES else None
 
         for i in range(TILES + LAG_FIN):
-            if at(i) is not None:
-                widen(at(i))
-            if at(i - LAG_SCALE) is not None:
-                scale_on_gpsimd(at(i - LAG_SCALE))
+            if i < EARLY:
+                widen(ORDER[i])
+            if at(i - LAG_GP) is not None:
+                scale_on_gpsimd(at(i - LAG_GP))
             if at(i - LAG_EVAC) is not None:
                 empty(at(i - LAG_EVAC))
+            if i - LAG_CAST >= EARLY and at(i - LAG_CAST) is not None and i > 0:
+                widen(at(i - LAG_CAST))
+            if i == TOKQ:
+                quantise_tokens()
             if at(i - LAG_MUL) is not None:
                 multiply(at(i - LAG_MUL), 0)
-            if i == 1:
-                turn_tokens()
-            if i == 3:
+            if at(i - LAG_FIN) is not None:
+                finish(at(i - LAG_FIN))
+            if i == TABLES:
                 make_tables()
             if at(i - LAG_TURN) is not None:
                 turn(at(i - LAG_TURN))
+            if i == TOK:
+                turn_tokens()
             if at(i - LAG_MUL) is not None:
                 multiply(at(i - LAG_MUL), 1)
             if at(i - LAG_ROPE) is not None:
                 rope_or_bias(at(i - LAG_ROPE))
-            if i == LAG_QUANT:
-                quantise_tokens()
             if at(i - LAG_QUANT) is not None:
                 quantise(at(i - LAG_QUANT))
-                if at(i) is not None and not on_bytes(at(i)):
+                if i + 1 - LAG_GP < TILES and not on_bytes(ORDER[i + 1 - LAG_GP]):
                     nc.gpsimd.memset(tiles[("w_packed", at(i - LAG_QUANT))][:, 0:2], 0.0)
             if at(i - LAG_FIN) is not None:
-                finish(at(i - LAG_FIN))
+                copy_out(at(i - LAG_FIN))

@@ -33,7 +33,6 @@ N_MOVING = COPIES * TOKENS
 GP_PASS = PASSES - 1
 
 ORDER = [j for pair in range(HEADS) for j in (2 * pair, 2 * pair + 1, 2 * HEADS + pair)]
-ORDER = ORDER[0 : TILES - 4] + ORDER[TILES - 3 : TILES - 1] + [ORDER[TILES - 4], ORDER[TILES - 1]]
 LAST = ORDER[TILES - 1]
 EARLY = 5
 
@@ -120,6 +119,14 @@ def tile_flashneoxattention_pa_kernel(
         bias = const.tile([P, TILES], F32, name="bias")
         tables = const.tile([P, COPIES, TOKENS], F32, name="tables")
 
+        warm_rows = const.tile([P, 512], BF16, name="warm_rows")
+        nc.gpsimd.memset(warm_rows[:], 0.0)
+        warm_bank = ps_sums.tile([P, 512], F32, name="warm_bank", tag="sums")
+
+        def warm(count):
+            for k in range(count):
+                nc.tensor.matmul(warm_bank[:], lhsT=ident_bf[:], rhs=warm_rows[:], start=True, stop=True)
+
         tiles = {}
 
         def on_bytes(j):
@@ -187,7 +194,7 @@ def tile_flashneoxattention_pa_kernel(
 
         def on_scalar(j):
             n = ORDER.index(j)
-            return n >= EARLY and has_rope(j)
+            return n >= EARLY and has_rope(j) and n % 9 != 4
 
         def scale_on_scalar(packed_words, bank, g, gl):
             planes = work.tile([P, 2, P, 2], BF16, name="planes", tag="planes")
@@ -394,14 +401,18 @@ def tile_flashneoxattention_pa_kernel(
                 quantise_tokens()
             if at(i - LAG_MUL) is not None:
                 multiply(at(i - LAG_MUL), 0)
-            if at(i - LAG_FIN) is not None:
-                finish(at(i - LAG_FIN))
             if i == TABLES:
                 make_tables()
+            if i == 0:
+                warm(6)
             if at(i - LAG_TURN) is not None:
+                if 1 <= i <= 3:
+                    warm(2)
                 turn(at(i - LAG_TURN))
             if i == TOK:
                 turn_tokens()
+            if at(i - LAG_FIN) is not None:
+                finish(at(i - LAG_FIN))
             if at(i - LAG_MUL) is not None:
                 multiply(at(i - LAG_MUL), 1)
             if at(i - LAG_ROPE) is not None:

@@ -34,11 +34,11 @@ GP_PASS = PASSES - 1
 
 ORDER = [j for pair in range(HEADS) for j in (2 * pair, 2 * pair + 1, 2 * HEADS + pair)]
 LAST = ORDER[TILES - 1]
-EARLY = 5
+EARLY = 2
 
-TOK = 2
-TOKQ = 3
-TABLES = 3
+TOK = 3
+TOKQ = 4
+TABLES = 4
 LAG_CAST = -2
 LAG_GP = 0
 LAG_TURN = 1
@@ -71,12 +71,8 @@ def tile_flashneoxattention_pa_kernel(
         ps_done = ctx.enter_context(tc.psum_pool(name="ps_done", bufs=2))
         ctx.enter_context(tc.manual_schedule())
 
-        scale_rows = const.tile([P, HID], F32, name="scale_rows")
+        scale_rows = const.tile([P, K_PASS], F32, name="scale_rows")
         scale_vec = w_qkv_scale.rearrange("o k -> (o k)")
-        for g in range(PASSES):
-            cols = slice(g * K_PASS, (g + 1) * K_PASS)
-            nc.scalar.dma_start(out=scale_rows[:, cols], in_=scale_vec[cols].partition_broadcast(P))
-
         scale_cols = const.tile([P, PASSES, PACK], F32, name="scale_cols")
         bias_rows = const.tile([P, P], BF16, name="bias_rows")
         nc.vector.memset(bias_rows[:], 0.0)
@@ -92,11 +88,19 @@ def tile_flashneoxattention_pa_kernel(
         x_rows = const.tile([P, 2, HID], BF16, name="x_rows")
         for n in range(TILES):
             j = ORDER[n]
-            if n == 3:
+            if n == 4:
                 nc.sync.dma_start(out=x_rows[:], in_=hidden_states.rearrange("(a p) k -> p a k", p=P))
-            nc.sync.dma_start(out=w_bytes[j][:], in_=w_qkv_bytes[j * P : (j + 1) * P, :])
-            if n == 2:
-                nc.sync.dma_start(out=scale_cols[:], in_=w_qkv_scale.rearrange("o (g p t) -> p (o g) t", p=P, t=PACK))
+            if n == 0:
+                for c in range(2):
+                    cols = slice(c * HID // 2, (c + 1) * HID // 2)
+                    nc.sync.dma_start(out=w_bytes[j][:, cols], in_=w_qkv_bytes[j * P : (j + 1) * P, cols])
+                    if c == 0:
+                        nc.sync.dma_start(out=scale_cols[:], in_=w_qkv_scale.rearrange("o (g p t) -> p (o g) t", p=P, t=PACK))
+            else:
+                nc.sync.dma_start(out=w_bytes[j][:], in_=w_qkv_bytes[j * P : (j + 1) * P, :])
+            if n == 1:
+                nc.sync.dma_start(out=scale_rows[:], in_=scale_vec[GP_PASS * K_PASS : HID].partition_broadcast(P))
+            if n == 4:
                 nc.sync.dma_start(out=bias_rows[0:TILES, :], in_=b_qkv.rearrange("(j p) -> j p", p=P))
                 nc.sync.dma_start(out=trig[:, :, 0, :], in_=cos_view)
                 nc.sync.dma_start(out=trig[:, :, 1, :], in_=cos_view)
@@ -115,6 +119,8 @@ def tile_flashneoxattention_pa_kernel(
 
         x_codes = const.tile([P, (PASSES + 1) * TOKENS], U32, name="x_codes", align_bytes=64)
         x_scales = const.tile([P, (PASSES + 1) * TOKENS], U8, name="x_scales", align_bytes=64)
+        nc.gpsimd.memset(x_codes[:, PASSES * TOKENS :], 0)
+        nc.gpsimd.memset(x_scales[:, PASSES * TOKENS :], 0)
         x_packed = const.tile([P, PASSES, TOKENS * PACK], BF16, name="x_packed", align_bytes=64)
         bias = const.tile([P, TILES], F32, name="bias")
         tables = const.tile([P, COPIES, TOKENS], F32, name="tables")
@@ -129,36 +135,27 @@ def tile_flashneoxattention_pa_kernel(
 
         tiles = {}
 
-        def on_bytes(j):
+        def all_on_vector(j):
             return j in ORDER[0:EARLY]
 
         def widen(j):
             w_rows = rows_pool.tile([P, HID], BF16, name="w_rows", tag="w_rows")
-            if on_bytes(j):
-                if j == ORDER[0]:
-                    tiles["first"] = w_rows
-                elif j == ORDER[1]:
-                    for g in range(PASSES):
-                        cols = slice(g * K_PASS, (g + 1) * K_PASS)
-                        for jj, dst in ((ORDER[0], tiles["first"]), (j, w_rows)):
-                            nc.vector.tensor_tensor(
-                                out=dst[:, cols], in0=w_bytes[jj][:, cols].bitcast(FP8), in1=scale_rows[:, cols], op=ALU.mult
-                            )
-                else:
-                    nc.vector.tensor_tensor(out=w_rows[:], in0=w_bytes[j][:].bitcast(FP8), in1=scale_rows[:], op=ALU.mult)
-            else:
-                nc.scalar.copy(out=w_rows[:], in_=w_bytes[j][:].bitcast(FP8))
+            pieces = 2 if j == ORDER[0] else 1
+            width = HID // pieces
+            for c in range(pieces):
+                cols = slice(c * width, (c + 1) * width)
+                nc.scalar.copy(out=w_rows[:, cols], in_=w_bytes[j][:, cols].bitcast(FP8))
             tiles[("w_rows", j)] = w_rows
 
         def scale_on_gpsimd(j):
-            if not on_bytes(j):
+            if not all_on_vector(j):
                 w_rows = tiles[("w_rows", j)]
                 cols = slice(GP_PASS * K_PASS, (GP_PASS + 1) * K_PASS)
                 w_gp = work.tile([P, K_PASS], BF16, name="w_gp", tag="w_gp")
                 nc.gpsimd.tensor_tensor(
                     out=w_gp[:].rearrange("p (u m e) -> p u m e", u=2, e=2),
                     in0=w_rows[:, cols].rearrange("p (m u e) -> p u m e", u=2, e=2),
-                    in1=scale_rows[:, cols].rearrange("p (m u e) -> p u m e", u=2, e=2),
+                    in1=scale_rows[:].rearrange("p (m u e) -> p u m e", u=2, e=2),
                     op=ALU.mult,
                 )
                 tiles[("w_gp", j)] = w_gp
@@ -174,7 +171,7 @@ def tile_flashneoxattention_pa_kernel(
                 for gl in range(2):
                     for u in range(2):
                         g = 2 * b + gl
-                        if g == GP_PASS and not on_bytes(j):
+                        if g == GP_PASS and not all_on_vector(j):
                             halves = tiles[("w_gp", j)][:].bitcast(F32)
                             nc.tensor.transpose(bank[:, u, gl, :], halves[:, u * P : (u + 1) * P], ident[:])
                         else:
@@ -194,7 +191,7 @@ def tile_flashneoxattention_pa_kernel(
 
         def on_scalar(j):
             n = ORDER.index(j)
-            return n >= EARLY and has_rope(j) and n % 9 != 4
+            return n >= EARLY and has_rope(j) and n % 9 != 0
 
         def scale_on_scalar(packed_words, bank, g, gl):
             planes = work.tile([P, 2, P, 2], BF16, name="planes", tag="planes")
@@ -215,11 +212,9 @@ def tile_flashneoxattention_pa_kernel(
             packed_words = w_packed[:].bitcast(F32).rearrange("p (g r u) -> p g r u", g=PASSES, u=2)
             packed_vals = w_packed[:].rearrange("p (g r u e) -> p g r u e", g=PASSES, u=2, e=2)
             banks = tiles[("banks", j)]
-            if on_bytes(j):
-                for b in range(2):
-                    nc.scalar.copy(
-                        out=packed_words[:, 2 * b : 2 * b + 2], in_=banks[b][:].rearrange("p u g r -> p g r u")
-                    )
+            if all_on_vector(j):
+                scale_on_vector(packed_vals, banks[0], 0, 0, 2)
+                scale_on_vector(packed_vals, banks[1], 2, 0, 2)
             else:
                 if on_scalar(j):
                     scale_on_scalar(packed_words, banks[1], 2, 0)
@@ -365,10 +360,10 @@ def tile_flashneoxattention_pa_kernel(
             nc.scalar.activation(out=trig[:, :, 3, :], in_=trig[:, :, 3, :], func=ACT.Copy, scale=-1.0)
 
         def quantise_tokens():
-            for block in range(PASSES + 1):
-                cols = slice(block * TOKENS, (block + 1) * TOKENS)
+            for g in range(PASSES):
+                cols = slice(g * TOKENS, (g + 1) * TOKENS)
                 nc.vector.quantize_mx(
-                    out=x_codes[:, cols].bitcast(FP8X4), scales=x_scales[:, cols], in_=x_packed[:, block % PASSES, :]
+                    out=x_codes[:, cols].bitcast(FP8X4), scales=x_scales[:, cols], in_=x_packed[:, g, :]
                 )
 
         def make_tables():
@@ -389,13 +384,14 @@ def tile_flashneoxattention_pa_kernel(
             return ORDER[n] if 0 <= n < TILES else None
 
         for i in range(TILES + LAG_FIN):
-            if i < EARLY:
-                widen(ORDER[i])
+            if i == 0:
+                for n in range(-LAG_CAST):
+                    widen(ORDER[n])
             if at(i - LAG_GP) is not None:
                 scale_on_gpsimd(at(i - LAG_GP))
             if at(i - LAG_EVAC) is not None:
                 empty(at(i - LAG_EVAC))
-            if i - LAG_CAST >= EARLY and at(i - LAG_CAST) is not None and i > 0:
+            if at(i - LAG_CAST) is not None:
                 widen(at(i - LAG_CAST))
             if i == TOKQ:
                 quantise_tokens()
@@ -404,22 +400,24 @@ def tile_flashneoxattention_pa_kernel(
             if i == TABLES:
                 make_tables()
             if i == 0:
-                warm(6)
+                warm(4)
             if at(i - LAG_TURN) is not None:
                 if 1 <= i <= 3:
                     warm(2)
                 turn(at(i - LAG_TURN))
             if i == TOK:
                 turn_tokens()
-            if at(i - LAG_FIN) is not None:
+            if at(i - LAG_FIN) is not None and i <= TILES:
                 finish(at(i - LAG_FIN))
             if at(i - LAG_MUL) is not None:
                 multiply(at(i - LAG_MUL), 1)
+            if at(i - LAG_FIN) is not None and i > TILES:
+                finish(at(i - LAG_FIN))
             if at(i - LAG_ROPE) is not None:
                 rope_or_bias(at(i - LAG_ROPE))
             if at(i - LAG_QUANT) is not None:
                 quantise(at(i - LAG_QUANT))
-                if i + 1 - LAG_GP < TILES and not on_bytes(ORDER[i + 1 - LAG_GP]):
+                if i + 1 - LAG_GP < TILES and not all_on_vector(ORDER[i + 1 - LAG_GP]):
                     nc.gpsimd.memset(tiles[("w_packed", at(i - LAG_QUANT))][:, 0:2], 0.0)
             if at(i - LAG_FIN) is not None:
                 copy_out(at(i - LAG_FIN))

@@ -91,8 +91,8 @@ def tile_flashneoxattention_pa_kernel(
             if n == 4:
                 nc.sync.dma_start(out=x_rows[:], in_=hidden_states.rearrange("(a p) k -> p a k", p=P))
             if n == 0:
-                for c in range(2):
-                    cols = slice(c * HID // 2, (c + 1) * HID // 2)
+                for c in range(PASSES):
+                    cols = slice(c * K_PASS, (c + 1) * K_PASS)
                     nc.sync.dma_start(out=w_bytes[j][:, cols], in_=w_qkv_bytes[j * P : (j + 1) * P, cols])
                     if c == 0:
                         nc.sync.dma_start(out=scale_cols[:], in_=w_qkv_scale.rearrange("o (g p t) -> p (o g) t", p=P, t=PACK))
@@ -140,7 +140,7 @@ def tile_flashneoxattention_pa_kernel(
 
         def widen(j):
             w_rows = rows_pool.tile([P, HID], BF16, name="w_rows", tag="w_rows")
-            pieces = 2 if j == ORDER[0] else 1
+            pieces = PASSES if j == ORDER[0] else 1
             width = HID // pieces
             for c in range(pieces):
                 cols = slice(c * width, (c + 1) * width)
@@ -163,14 +163,18 @@ def tile_flashneoxattention_pa_kernel(
         def transpose_pass(dst, words, g, u):
             nc.tensor.transpose(dst, words[:, WORDS_PASS * g + u : WORDS_PASS * (g + 1) : 2], ident[:])
 
+        def passes_a_bank(j):
+            return 1 if j == ORDER[0] else 2
+
         def turn(j):
             words = tiles[("w_rows", j)][:].bitcast(F32)
             banks = []
-            for b in range(2):
-                bank = ps_words.tile([P, 2, 2, P], F32, name="bank", tag="words")
-                for gl in range(2):
+            held = passes_a_bank(j)
+            for b in range(PASSES // held):
+                bank = ps_words.tile([P, 2, held, P], F32, name="bank", tag="words")
+                for gl in range(held):
                     for u in range(2):
-                        g = 2 * b + gl
+                        g = held * b + gl
                         if g == GP_PASS and not all_on_vector(j):
                             halves = tiles[("w_gp", j)][:].bitcast(F32)
                             nc.tensor.transpose(bank[:, u, gl, :], halves[:, u * P : (u + 1) * P], ident[:])
@@ -191,7 +195,7 @@ def tile_flashneoxattention_pa_kernel(
 
         def on_scalar(j):
             n = ORDER.index(j)
-            return n >= EARLY and has_rope(j) and n % 9 != 0
+            return n >= EARLY and has_rope(j) and n % 12 != 0
 
         def scale_on_scalar(packed_words, bank, g, gl):
             planes = work.tile([P, 2, P, 2], BF16, name="planes", tag="planes")
@@ -213,8 +217,9 @@ def tile_flashneoxattention_pa_kernel(
             packed_vals = w_packed[:].rearrange("p (g r u e) -> p g r u e", g=PASSES, u=2, e=2)
             banks = tiles[("banks", j)]
             if all_on_vector(j):
-                scale_on_vector(packed_vals, banks[0], 0, 0, 2)
-                scale_on_vector(packed_vals, banks[1], 2, 0, 2)
+                held = passes_a_bank(j)
+                for b in range(PASSES // held):
+                    scale_on_vector(packed_vals, banks[b], held * b, 0, held)
             else:
                 if on_scalar(j):
                     scale_on_scalar(packed_words, banks[1], 2, 0)
@@ -395,15 +400,17 @@ def tile_flashneoxattention_pa_kernel(
                 widen(at(i - LAG_CAST))
             if i == TOKQ:
                 quantise_tokens()
+            if i <= 4 and at(i - LAG_TURN) is not None:
+                if 2 <= i <= 3:
+                    warm(2)
+                turn(at(i - LAG_TURN))
             if at(i - LAG_MUL) is not None:
                 multiply(at(i - LAG_MUL), 0)
             if i == TABLES:
                 make_tables()
             if i == 0:
                 warm(4)
-            if at(i - LAG_TURN) is not None:
-                if 1 <= i <= 3:
-                    warm(2)
+            if i > 4 and at(i - LAG_TURN) is not None:
                 turn(at(i - LAG_TURN))
             if i == TOK:
                 turn_tokens()

@@ -197,18 +197,18 @@ def tile_flashneoxattention_pa_kernel(
             n = ORDER.index(j)
             return n >= EARLY and has_rope(j) and n % 12 != 0
 
-        def scale_on_scalar(packed_words, bank, g, gl):
-            planes = work.tile([P, 2, P, 2], BF16, name="planes", tag="planes")
+        def scale_on_scalar(packed_vals, bank, g, gl):
+            planes = work.tile([P, PACK, P], BF16, name="planes", tag="planes")
             for t in range(PACK):
                 nc.scalar.activation(
-                    out=planes[:, t // 2, :, t % 2],
+                    out=planes[:, t, :],
                     in_=bank[:, t // 2, gl, :].bitcast(BF16).rearrange("p (r e) -> p r e", e=2)[:, :, t % 2],
                     func=ACT.Copy,
                     scale=scale_cols[:, g, t : t + 1],
                 )
             nc.scalar.copy(
-                out=packed_words[:, g],
-                in_=planes[:].rearrange("p u r e -> p u (r e)").bitcast(F32).rearrange("p u r -> p r u"),
+                out=packed_vals[:, g].rearrange("p (c i) u e -> p c (u e) i", i=4),
+                in_=planes[:].rearrange("p t (c i) -> p c t i", i=4),
             )
 
         def empty(j):
@@ -222,7 +222,7 @@ def tile_flashneoxattention_pa_kernel(
                     scale_on_vector(packed_vals, banks[b], held * b, 0, held)
             else:
                 if on_scalar(j):
-                    scale_on_scalar(packed_words, banks[1], 2, 0)
+                    scale_on_scalar(packed_vals, banks[1], 2, 0)
                 else:
                     scale_on_vector(packed_vals, banks[1], 2, 0, 1)
                 scale_on_vector(packed_vals, banks[0], 0, 0, 2)

from contextlib import ExitStack

import concourse.mybir as mybir
from concourse.masks import make_identity

TOKENS = 256
HID = 2048
HEADS = 16
D = 128
HALF = D // 2
TILES = 3 * HEADS

FLOPS = 2 * TOKENS * 3 * HID * HID

F32 = mybir.dt.float32
BF16 = mybir.dt.bfloat16
U32 = mybir.dt.uint32
U8 = mybir.dt.uint8
FP8 = mybir.dt.float8_e4m3fn
FP8X4 = mybir.dt.float8_e4m3fn_x4
ACT = mybir.ActivationFunctionType
ALU = mybir.AluOpType

P = 128
PACK = 4
K_PASS = P * PACK
PASSES = HID // K_PASS
WORDS_PASS = K_PASS // 2
GROUP = 4
TOKEN_TILES = TOKENS // P
COPIES = 2
N_MOVING = COPIES * TOKENS
GP_PASS = PASSES - 1

ORDER = [j for pair in range(HEADS) for j in (2 * pair, 2 * pair + 1, 2 * HEADS + pair)]
LAST = ORDER[TILES - 1]
EARLY = 2

TOK = 3
TOKQ = 4
TABLES = 4
LAG_CAST = -2
LAG_GP = 0
LAG_TURN = 1
LAG_EVAC = 2
LAG_QUANT = 3
LAG_MUL = 4
LAG_ROPE = 5
LAG_FIN = 6


def has_rope(j):
    return j < 2 * HEADS


def tile_flashneoxattention_pa_kernel(
    tc, hidden_states, cos, sin, w_qkv_bytes, w_qkv_scale, b_qkv, out_0, out_1, out_2
):
    nc = tc.nc
    outs = (out_0, out_1, out_2)

    with ExitStack() as ctx:
        const = ctx.enter_context(tc.tile_pool(name="const", bufs=1))
        byte_pool = ctx.enter_context(tc.tile_pool(name="byte_pool", bufs=TILES))
        work = ctx.enter_context(tc.tile_pool(name="work", bufs=4))
        rows_pool = ctx.enter_context(tc.tile_pool(name="rows_pool", bufs=6))
        v_pool = ctx.enter_context(tc.tile_pool(name="v_pool", bufs=2))
        stage_pool = ctx.enter_context(tc.tile_pool(name="stage_pool", bufs=3))
        ps_words = ctx.enter_context(tc.psum_pool(name="ps_words", bufs=4))
        ps_sums = ctx.enter_context(tc.psum_pool(name="ps_sums", bufs=2))
        ps_done = ctx.enter_context(tc.psum_pool(name="ps_done", bufs=2))
        ctx.enter_context(tc.manual_schedule())

        scale_rows = const.tile([P, K_PASS], F32, name="scale_rows")
        scale_vec = w_qkv_scale.rearrange("o k -> (o k)")
        scale_cols = const.tile([P, PASSES, PACK], F32, name="scale_cols")
        bias_rows = const.tile([P, P], BF16, name="bias_rows")
        nc.vector.memset(bias_rows[:], 0.0)
        bias_v = const.tile([P, HEADS * D], BF16, name="bias_v")
        trig = const.tile([P, 2, 4, HALF], BF16, name="trig")
        cos_view = cos.rearrange("(a p) d -> p a d", p=P)
        sin_view = sin.rearrange("(a p) d -> p a d", p=P)

        w_bytes = {}
        for j in ORDER:
            byte_tile = byte_pool.tile([P, HID], U8, name="byte_tile", tag="w_bytes")
            w_bytes[j] = byte_tile
        x_rows = const.tile([P, 2, HID], BF16, name="x_rows")
        for n in range(TILES):
            j = ORDER[n]
            if n == 4:
                nc.sync.dma_start(out=x_rows[:], in_=hidden_states.rearrange("(a p) k -> p a k", p=P))
            if n == 0:
                for c in range(PASSES):
                    cols = slice(c * K_PASS, (c + 1) * K_PASS)
                    nc.sync.dma_start(out=w_bytes[j][:, cols], in_=w_qkv_bytes[j * P : (j + 1) * P, cols])
                    if c == 0:
                        nc.sync.dma_start(out=scale_cols[:], in_=w_qkv_scale.rearrange("o (g p t) -> p (o g) t", p=P, t=PACK))
            else:
                nc.sync.dma_start(out=w_bytes[j][:], in_=w_qkv_bytes[j * P : (j + 1) * P, :])
            if n == 1:
                nc.sync.dma_start(out=scale_rows[:], in_=scale_vec[GP_PASS * K_PASS : HID].partition_broadcast(P))
            if n == 4:
                nc.sync.dma_start(out=bias_rows[0:TILES, :], in_=b_qkv.rearrange("(j p) -> j p", p=P))
                nc.sync.dma_start(out=trig[:, :, 0, :], in_=cos_view)
                nc.sync.dma_start(out=trig[:, :, 1, :], in_=cos_view)
                nc.sync.dma_start(out=trig[:, :, 2, :], in_=sin_view)
                nc.sync.dma_start(out=trig[:, :, 3, :], in_=sin_view)
            if n == 5:
                nc.sync.dma_start(out=bias_v[:], in_=b_qkv[2 * HEADS * D : 3 * HEADS * D].partition_broadcast(P))

        ident = const.tile([P, P], F32, name="ident")
        make_identity(nc, ident[:])
        ident_bf = const.tile([P, P], BF16, name="ident_bf")
        make_identity(nc, ident_bf[:])
        swap_halves = const.tile([P, P], F32, name="swap_halves")
        nc.vector.tensor_copy(out=swap_halves[:, 0:HALF], in_=ident[:, HALF:P])
        nc.vector.tensor_copy(out=swap_halves[:, HALF:P], in_=ident[:, 0:HALF])

        x_codes = const.tile([P, (PASSES + 1) * TOKENS], U32, name="x_codes", align_bytes=64)
        x_scales = const.tile([P, (PASSES + 1) * TOKENS], U8, name="x_scales", align_bytes=64)
        nc.gpsimd.memset(x_codes[:, PASSES * TOKENS :], 0)
        nc.gpsimd.memset(x_scales[:, PASSES * TOKENS :], 0)
        x_packed = const.tile([P, PASSES, TOKENS * PACK], BF16, name="x_packed", align_bytes=64)
        bias = const.tile([P, TILES], F32, name="bias")
        tables = const.tile([P, COPIES, TOKENS], F32, name="tables")

        warm_rows = const.tile([P, 512], BF16, name="warm_rows")
        nc.gpsimd.memset(warm_rows[:], 0.0)
        warm_bank = ps_sums.tile([P, 512], F32, name="warm_bank", tag="sums")

        def warm(count):
            for k in range(count):
                nc.tensor.matmul(warm_bank[:], lhsT=ident_bf[:], rhs=warm_rows[:], start=True, stop=True)

        tiles = {}

        def all_on_vector(j):
            return j in ORDER[0:EARLY]

        def widen(j):
            w_rows = rows_pool.tile([P, HID], BF16, name="w_rows", tag="w_rows")
            pieces = PASSES if j == ORDER[0] else 1
            width = HID // pieces
            for c in range(pieces):
                cols = slice(c * width, (c + 1) * width)
                nc.scalar.copy(out=w_rows[:, cols], in_=w_bytes[j][:, cols].bitcast(FP8))
            tiles[("w_rows", j)] = w_rows

        def scale_on_gpsimd(j):
            if not all_on_vector(j):
                w_rows = tiles[("w_rows", j)]
                cols = slice(GP_PASS * K_PASS, (GP_PASS + 1) * K_PASS)
                w_gp = work.tile([P, K_PASS], BF16, name="w_gp", tag="w_gp")
                nc.gpsimd.tensor_tensor(
                    out=w_gp[:].rearrange("p (u m e) -> p u m e", u=2, e=2),
                    in0=w_rows[:, cols].rearrange("p (m u e) -> p u m e", u=2, e=2),
                    in1=scale_rows[:].rearrange("p (m u e) -> p u m e", u=2, e=2),
                    op=ALU.mult,
                )
                tiles[("w_gp", j)] = w_gp

        def transpose_pass(dst, words, g, u):
            nc.tensor.transpose(dst, words[:, WORDS_PASS * g + u : WORDS_PASS * (g + 1) : 2], ident[:])

        def passes_a_bank(j):
            return 1 if j == ORDER[0] else 2

        def turn(j):
            words = tiles[("w_rows", j)][:].bitcast(F32)
            banks = []
            held = passes_a_bank(j)
            for b in range(PASSES // held):
                bank = ps_words.tile([P, 2, held, P], F32, name="bank", tag="words")
                for gl in range(held):
                    for u in range(2):
                        g = held * b + gl
                        if g == GP_PASS and not all_on_vector(j):
                            halves = tiles[("w_gp", j)][:].bitcast(F32)
                            nc.tensor.transpose(bank[:, u, gl, :], halves[:, u * P : (u + 1) * P], ident[:])
                        else:
                            transpose_pass(bank[:, u, gl, :], words, g, u)
                banks.append(bank)
            tiles[("banks", j)] = banks

        def scale_on_vector(packed, bank, g, gl, count):
            vals = bank[:, :, gl : gl + count, :].bitcast(BF16).rearrange("p u g (r e) -> p g r u e", e=2)
            scales = (
                scale_cols[:, g : g + count, :]
                .rearrange("p g (u e) -> p g u e", e=2)
                .unsqueeze(2)
                .to_broadcast([P, count, P, 2, 2])
            )
            nc.vector.tensor_tensor(out=packed[:, g : g + count], in0=vals, in1=scales, op=ALU.mult)

        def on_scalar(j):
            n = ORDER.index(j)
            return n >= EARLY and has_rope(j) and n % 12 != 0

        def scale_on_scalar(packed_vals, bank, g, gl):
            planes = work.tile([P, PACK, P], BF16, name="planes", tag="planes")
            for t in range(PACK):
                nc.scalar.activation(
                    out=planes[:, t, :],
                    in_=bank[:, t // 2, gl, :].bitcast(BF16).rearrange("p (r e) -> p r e", e=2)[:, :, t % 2],
                    func=ACT.Copy,
                    scale=scale_cols[:, g, t : t + 1],
                )
            nc.scalar.copy(
                out=packed_vals[:, g].rearrange("p (c i) u e -> p c (u e) i", i=4),
                in_=planes[:].rearrange("p t (c i) -> p c t i", i=4),
            )

        def empty(j):
            w_packed = work.tile([P, PASSES * P * PACK], BF16, name="w_packed", tag="w_packed", align_bytes=64)
            packed_words = w_packed[:].bitcast(F32).rearrange("p (g r u) -> p g r u", g=PASSES, u=2)
            packed_vals = w_packed[:].rearrange("p (g r u e) -> p g r u e", g=PASSES, u=2, e=2)
            banks = tiles[("banks", j)]
            if all_on_vector(j):
                held = passes_a_bank(j)
                for b in range(PASSES // held):
                    scale_on_vector(packed_vals, banks[b], held * b, 0, held)
            else:
                if on_scalar(j):
                    scale_on_scalar(packed_vals, banks[1], 2, 0)
                else:
                    scale_on_vector(packed_vals, banks[1], 2, 0, 1)
                scale_on_vector(packed_vals, banks[0], 0, 0, 2)
                nc.scalar.copy(out=packed_words[:, GP_PASS], in_=banks[1][:, :, 1, :].rearrange("p u r -> p r u"))
            tiles[("w_packed", j)] = w_packed

        def quantise(j):
            w_codes = work.tile([P, PASSES * P], U32, name="w_codes", tag="w_codes", align_bytes=64)
            w_scales = work.tile([P, PASSES * P], U8, name="w_scales", tag="w_scales", align_bytes=64)
            nc.vector.quantize_mx(
                out=w_codes[:].bitcast(FP8X4), scales=w_scales[:], in_=tiles[("w_packed", j)][:]
            )
            tiles[("w_codes", j)] = (w_codes, w_scales)

        def multiply(j, half):
            w_codes, w_scales = tiles[("w_codes", j)]
            if half == 0:
                new_sums = ps_sums.tile([P, N_MOVING], F32, name="new_sums", tag="sums")
                tiles[("sums", j)] = new_sums
            sums = tiles[("sums", j)]
            if has_rope(j):
                for g in (2 * half, 2 * half + 1):
                    rows = slice(g * P, (g + 1) * P)
                    toks = slice(g * TOKENS, g * TOKENS + N_MOVING)
                    nc.tensor.matmul_mx(
                        out=sums[:],
                        lhsT=w_codes[:, rows].bitcast(FP8X4),
                        lhsT_scale=w_scales[:, rows],
                        rhs=x_codes[:, toks].bitcast(FP8X4),
                        rhs_scale=x_scales[:, toks],
                        start=(g == 0),
                        stop=(g == PASSES - 1),
                    )
            else:
                for g in range(PASSES):
                    rows = slice(g * P, (g + 1) * P)
                    toks = slice(g * TOKENS + half * P, g * TOKENS + (half + 1) * P)
                    nc.tensor.matmul_mx(
                        out=sums[:, half * D : (half + 1) * D],
                        lhsT=x_codes[:, toks].bitcast(FP8X4),
                        lhsT_scale=x_scales[:, toks],
                        rhs=w_codes[:, rows].bitcast(FP8X4),
                        rhs_scale=w_scales[:, rows],
                        start=(g == 0),
                        stop=(g == PASSES - 1),
                    )

        def store_heads(queue, j, count, a, staged):
            first_head = (j % HEADS) - (count - 1)
            queue.dma_start(
                out=outs[j // HEADS][a * P : (a + 1) * P, first_head : first_head + count, :].rearrange(
                    "t h d -> t (h d)"
                ),
                in_=staged,
            )

        def rope_or_bias(j):
            sums = tiles[("sums", j)]
            if has_rope(j):
                products = work.tile([P, COPIES, TOKENS], F32, name="products", tag="products")
                nc.vector.scalar_tensor_tensor(
                    out=products[:],
                    in0=sums[:, 0:TOKENS].unsqueeze(1).to_broadcast([P, COPIES, TOKENS]),
                    scalar=bias[:, j : j + 1],
                    in1=tables[:],
                    op0=ALU.add,
                    op1=ALU.mult,
                )
                tiles[("products", j)] = products
            else:
                h = j - 2 * HEADS
                place = j % GROUP
                if place == 0:
                    new_stage = v_pool.tile([P, TOKEN_TILES, GROUP * D], F32, name="new_stage", tag="v_stage")
                    tiles["v_stage"] = new_stage
                stage = tiles["v_stage"]
                cols = slice(place * D, (place + 1) * D)
                nc.vector.tensor_tensor(
                    out=stage[:, :, cols],
                    in0=sums[:, 0:TOKENS].rearrange("p (a d) -> p a d", a=TOKEN_TILES),
                    in1=bias_v[:, h * D : (h + 1) * D].unsqueeze(1).to_broadcast([P, TOKEN_TILES, D]),
                    op=ALU.add,
                )
                if j == LAST - 1:
                    for a in range(TOKEN_TILES):
                        store_heads(nc.sync, j, GROUP - 1, a, stage[:, a, 0 : (GROUP - 1) * D])
                elif j == LAST:
                    store_heads(nc.sync, j, 1, 0, stage[:, 0, cols])
                    store_heads(nc.scalar, j, 1, 1, stage[:, 1, cols])
                elif place == GROUP - 1:
                    for a in range(TOKEN_TILES):
                        store_heads(nc.sync, j, GROUP, a, stage[:, a, :])

        def finish(j):
            if not has_rope(j):
                return
            place = j % GROUP
            if place == 0:
                new_stage = stage_pool.tile([P, TOKEN_TILES, GROUP * D], F32, name="new_stage", tag="rope_stage")
                tiles["rope_stage"] = new_stage
            stage = tiles["rope_stage"]
            done = ps_done.tile([P, TOKEN_TILES, D], F32, name="done", tag="done")
            products = tiles[("products", j)]
            for a in range(TOKEN_TILES):
                toks = slice(a * P, (a + 1) * P)
                nc.tensor.matmul(
                    done[:, a, :], lhsT=products[:, 0, toks], rhs=ident[:], is_transpose=True, start=True, stop=False
                )
                nc.tensor.matmul(
                    done[:, a, :],
                    lhsT=products[:, 1, toks],
                    rhs=swap_halves[:],
                    is_transpose=True,
                    start=False,
                    stop=True,
                )
            tiles[("done", j)] = (done, stage)

        def copy_out(j):
            if not has_rope(j):
                return
            done, stage = tiles[("done", j)]
            place = j % GROUP
            nc.scalar.copy(out=stage[:, :, place * D : (place + 1) * D], in_=done[:])
            if place == GROUP - 1:
                for a in range(TOKEN_TILES):
                    store_heads(nc.sync, j, GROUP, a, stage[:, a, :])

        def turn_tokens():
            for g in range(PASSES):
                bank = ps_words.tile([P, 2, TOKENS], F32, name="bank", tag="words")
                for a in range(2):
                    words = x_rows[:, a, :].bitcast(F32)
                    for u in range(2):
                        transpose_pass(bank[:, u, a * P : (a + 1) * P], words, g, u)
                nc.scalar.copy(
                    out=x_packed[:, g, :].bitcast(F32).rearrange("p (r u) -> p r u", u=2),
                    in_=bank[:].rearrange("p u r -> p r u"),
                )
            nc.scalar.activation(out=trig[:, :, 3, :], in_=trig[:, :, 3, :], func=ACT.Copy, scale=-1.0)

        def quantise_tokens():
            for g in range(PASSES):
                cols = slice(g * TOKENS, (g + 1) * TOKENS)
                nc.vector.quantize_mx(
                    out=x_codes[:, cols].bitcast(FP8X4), scales=x_scales[:, cols], in_=x_packed[:, g, :]
                )

        def make_tables():
            bias_bank = ps_words.tile([P, P], BF16, name="bias_bank", tag="words")
            nc.tensor.transpose(bias_bank[:], bias_rows[:], ident_bf[:])
            nc.scalar.copy(out=bias[:], in_=bias_bank[:, 0:TILES])
            trig_bank = ps_words.tile([P, COPIES, TOKENS], BF16, name="trig_bank", tag="words")
            for c in range(COPIES):
                for a in range(2):
                    nc.tensor.transpose(
                        trig_bank[:, c, a * P : (a + 1) * P],
                        trig[:, a, 2 * c : 2 * c + 2, :].rearrange("p c d -> p (c d)"),
                        ident_bf[:],
                    )
            nc.scalar.copy(out=tables[:], in_=trig_bank[:])

        def at(n):
            return ORDER[n] if 0 <= n < TILES else None

        for i in range(TILES + LAG_FIN):
            if i == 0:
                for n in range(-LAG_CAST):
                    widen(ORDER[n])
            if at(i - LAG_GP) is not None:
                scale_on_gpsimd(at(i - LAG_GP))
            if at(i - LAG_EVAC) is not None:
                empty(at(i - LAG_EVAC))
            if at(i - LAG_CAST) is not None:
                widen(at(i - LAG_CAST))
            if i == TOKQ:
                quantise_tokens()
            if i <= 4 and at(i - LAG_TURN) is not None:
                if 2 <= i <= 3:
                    warm(2)
                turn(at(i - LAG_TURN))
            if at(i - LAG_MUL) is not None:
                multiply(at(i - LAG_MUL), 0)
            if i == TABLES:
                make_tables()
            if i == 0:
                warm(4)
            if i > 4 and at(i - LAG_TURN) is not None:
                turn(at(i - LAG_TURN))
            if i == TOK:
                turn_tokens()
            if at(i - LAG_FIN) is not None and i <= TILES:
                finish(at(i - LAG_FIN))
            if at(i - LAG_MUL) is not None:
                multiply(at(i - LAG_MUL), 1)
            if at(i - LAG_FIN) is not None and i > TILES:
                finish(at(i - LAG_FIN))
            if at(i - LAG_ROPE) is not None:
                rope_or_bias(at(i - LAG_ROPE))
            if at(i - LAG_QUANT) is not None:
                quantise(at(i - LAG_QUANT))
                if i + 1 - LAG_GP < TILES and not all_on_vector(ORDER[i + 1 - LAG_GP]):
                    nc.gpsimd.memset(tiles[("w_packed", at(i - LAG_QUANT))][:, 0:2], 0.0)
            if at(i - LAG_FIN) is not None:
                copy_out(at(i - LAG_FIN))
